import numpy as np
import ml_dtypes

BF16 = ml_dtypes.bfloat16


def bf(x):
    return np.asarray(x, np.float32).astype(BF16)


def f32(x):
    return np.asarray(x, np.float32)


def f64(x):
    return np.asarray(x).astype(np.float64)


def striped(idx):
    return np.tile(idx.reshape(-1, 16).T, (8, 1))


C, S, N, M, CARD = 512, 4096, 1024, 3, 4
LOG_2PI = np.log(2.0 * np.pi)


def setup_inputs():
    return {"x": f32(np.random.standard_normal((C, S))), "means": f32(np.random.standard_normal((M, N))), "stds": f32(np.random.uniform(0.5, 1.5, (M, N))), "w1": f32(np.random.standard_normal((M, N))), "offs": striped(np.random.permutation(S)[:N])}


def reference(x, means, stds, w1, offs):
    idx = offs[:16].T.reshape(-1)
    xp = f64(x)[:, idx]
    mu, sd, w = f64(means), f64(stds), f64(w1)
    logw = w - np.log(np.exp(w).sum(axis=0, keepdims=True))
    z = (xp[:, None, :] + (-mu)[None]) / sd[None]
    t = -0.5 * z * z - np.log(sd)[None] - 0.5 * LOG_2PI + logw[None]
    top = t.max(axis=1, keepdims=True)
    y = top[:, 0, :] + np.log(np.exp(t - top).sum(axis=1))
    return y.reshape(C, N // CARD, CARD).sum(axis=2)

@@ -1,0 +1,99 @@
+import math
+
+import concourse.mybir as mybir
+
+F32 = mybir.dt.float32
+U16 = mybir.dt.uint16
+ALU = mybir.AluOpType
+FUNC = mybir.ActivationFunctionType
+
+P = 128
+C, S, N, M, CARD = 512, 4096, 1024, 3, 4
+HALF_LOG_2PI = 0.5 * math.log(2.0 * math.pi)
+
+
+def tile_spnneuronbig_kernel(tc, x, means, stds, w1, offs, out):
+    nc = tc.nc
+    with (
+        tc.tile_pool(name="held", bufs=1) as held,
+        tc.tile_pool(name="tables", bufs=C // P) as tables,
+        tc.tile_pool(name="work", bufs=2) as work,
+    ):
+        offsets = held.tile([P, N // 16], U16, name="offsets")
+        nc.sync.dma_start(offsets[:], offs)
+
+        mu = held.tile([P, M * N], F32, name="mu")
+        sd = held.tile([P, M * N], F32, name="sd")
+        w = held.tile([P, M * N], F32, name="w")
+        nc.scalar.dma_start(mu[:], means.rearrange("m n -> (m n)").partition_broadcast(P))
+        nc.gpsimd.dma_start(sd[:], stds.rearrange("m n -> (m n)").partition_broadcast(P))
+        nc.gpsimd.dma_start(w[:], w1.rearrange("m n -> (m n)").partition_broadcast(P))
+
+        windows = []
+        for b in range(C // P):
+            window = tables.tile([P, S], F32, name="window")
+            nc.sync.dma_start(window[:], x[b * P : (b + 1) * P, :])
+            windows.append(window)
+
+        def by_leaf(tile):
+            return tile[:].rearrange("p (m n) -> p m n", m=M)
+
+        def for_all_leaves(tile):
+            return tile[:].unsqueeze(1).to_broadcast([P, M, N])
+
+        def leaf(tile, m):
+            return tile[:, m * N : (m + 1) * N]
+
+        neg_mu = held.tile([P, M * N], F32, name="neg_mu")
+        nc.vector.tensor_scalar_mul(neg_mu[:], mu[:], -1.0)
+
+        inv_sd = held.tile([P, M * N], F32, name="inv_sd")
+        nc.vector.reciprocal(inv_sd[:], sd[:])
+
+        wmax = held.tile([P, N], F32, name="wmax")
+        nc.vector.tensor_max(wmax[:], leaf(w, 0), leaf(w, 1))
+        nc.vector.tensor_max(wmax[:], wmax[:], leaf(w, 2))
+        nc.vector.tensor_tensor(by_leaf(w), by_leaf(w), for_all_leaves(wmax), ALU.subtract)
+        exp_w = held.tile([P, M * N], F32, name="exp_w")
+        nc.scalar.activation(exp_w[:], w[:], FUNC.Exp)
+        wsum = held.tile([P, N], F32, name="wsum")
+        nc.vector.tensor_add(wsum[:], leaf(exp_w, 0), leaf(exp_w, 1))
+        nc.vector.tensor_add(wsum[:], wsum[:], leaf(exp_w, 2))
+        log_wsum = held.tile([P, N], F32, name="log_wsum")
+        nc.scalar.activation(log_wsum[:], wsum[:], FUNC.Ln)
+        log_sd = held.tile([P, M * N], F32, name="log_sd")
+        nc.scalar.activation(log_sd[:], sd[:], FUNC.Ln)
+
+        k = held.tile([P, M * N], F32, name="k")
+        nc.vector.tensor_sub(k[:], w[:], log_sd[:])
+        nc.vector.scalar_tensor_tensor(
+            by_leaf(k), by_leaf(k), HALF_LOG_2PI, for_all_leaves(log_wsum), ALU.subtract, ALU.subtract
+        )
+
+        for b in range(C // P):
+            term = work.tile([P, M * N], F32, name="term")
+            for m in range(M):
+                nc.vector.tensor_tensor(
+                    leaf(term, m), windows[b][:].indirect(offsets[:]), leaf(neg_mu, m), ALU.add
+                )
+            nc.vector.tensor_mul(term[:], term[:], inv_sd[:])
+            nc.scalar.activation(term[:], term[:], FUNC.Square, scale=math.sqrt(0.5))
+            nc.vector.tensor_sub(term[:], k[:], term[:])
+
+            top = work.tile([P, N], F32, name="top")
+            nc.vector.tensor_max(top[:], leaf(term, 0), leaf(term, 1))
+            nc.vector.tensor_max(top[:], top[:], leaf(term, 2))
+            nc.vector.tensor_tensor(by_leaf(term), by_leaf(term), for_all_leaves(top), ALU.subtract)
+            nc.scalar.activation(term[:], term[:], FUNC.Exp)
+
+            mix = work.tile([P, N], F32, name="mix")
+            nc.vector.tensor_add(mix[:], leaf(term, 0), leaf(term, 1))
+            nc.vector.tensor_add(mix[:], mix[:], leaf(term, 2))
+            nc.scalar.activation(mix[:], mix[:], FUNC.Ln)
+            nc.vector.tensor_add(mix[:], mix[:], top[:])
+
+            product = work.tile([P, N // CARD], F32, name="product")
+            nc.vector.reduce_sum(
+                product[:], mix[:].rearrange("p (q t) -> p q t", t=CARD), axis=mybir.AxisListType.X
+            )
+            nc.sync.dma_start(out[b * P : (b + 1) * P, :], product[:])

@@ -1,8 +1,10 @@
 import math
 
 import concourse.mybir as mybir
+from concourse.masks import make_block_diagonal, make_identity
 
 F32 = mybir.dt.float32
+BF16 = mybir.dt.bfloat16
 U16 = mybir.dt.uint16
 ALU = mybir.AluOpType
 FUNC = mybir.ActivationFunctionType
@@ -11,89 +13,208 @@ P = 128
 C, S, N, M, CARD = 512, 4096, 1024, 3, 4
 HALF_LOG_2PI = 0.5 * math.log(2.0 * math.pi)
 
+BLOCKS = C // P
+PIECE = 512
+PIECES = N // PIECE
+SUBS = PIECE // P
+COLS = N // P
+GROUPS = P // CARD
+CHUNKS = BLOCKS * PIECES
+BATCH = 2 * PIECES
+
 
 def tile_spnneuronbig_kernel(tc, x, means, stds, w1, offs, out):
     nc = tc.nc
     with (
         tc.tile_pool(name="held", bufs=1) as held,
-        tc.tile_pool(name="tables", bufs=C // P) as tables,
-        tc.tile_pool(name="work", bufs=2) as work,
+        tc.tile_pool(name="tables", bufs=BLOCKS) as tables,
+        tc.tile_pool(name="short", bufs=3) as short,
+        tc.tile_pool(name="long", bufs=5) as long,
+        tc.tile_pool(name="kept", bufs=CHUNKS) as kept,
+        tc.psum_pool(name="flipped", bufs=3) as flipped,
+        tc.psum_pool(name="sums", bufs=BATCH) as sums,
+        tc.psum_pool(name="products", bufs=1) as products,
     ):
         offsets = held.tile([P, N // 16], U16, name="offsets")
         nc.sync.dma_start(offsets[:], offs)
 
+        rows = held.tile([P, P], F32, name="rows")
+        nc.vector.memset(rows[:], 1.0)
+        nc.scalar.dma_start(rows[0 : M * COLS, :], stds.rearrange("m (b p) -> (m b) p", p=P))
+        nc.scalar.dma_start(rows[32 : 32 + M * COLS, :], w1.rearrange("m (b p) -> (m b) p", p=P))
+
         mu = held.tile([P, M * N], F32, name="mu")
-        sd = held.tile([P, M * N], F32, name="sd")
-        w = held.tile([P, M * N], F32, name="w")
-        nc.scalar.dma_start(mu[:], means.rearrange("m n -> (m n)").partition_broadcast(P))
-        nc.gpsimd.dma_start(sd[:], stds.rearrange("m n -> (m n)").partition_broadcast(P))
-        nc.gpsimd.dma_start(w[:], w1.rearrange("m n -> (m n)").partition_broadcast(P))
+        windows = [tables.tile([P, S], F32, name="window") for b in range(BLOCKS)]
 
-        windows = []
-        for b in range(C // P):
-            window = tables.tile([P, S], F32, name="window")
-            nc.sync.dma_start(window[:], x[b * P : (b + 1) * P, :])
-            windows.append(window)
+        def load_means(m):
+            nc.sync.dma_start(mu[:, m * N : (m + 1) * N], means[m, :].partition_broadcast(P))
 
-        def by_leaf(tile):
-            return tile[:].rearrange("p (m n) -> p m n", m=M)
+        def load_block(b):
+            nc.sync.dma_start(windows[b][:], x[b * P : (b + 1) * P, :])
 
-        def for_all_leaves(tile):
-            return tile[:].unsqueeze(1).to_broadcast([P, M, N])
+        load_means(0)
+        load_block(0)
+        for m in range(1, M):
+            load_means(m)
+        for b in range(1, BLOCKS):
+            load_block(b)
 
-        def leaf(tile, m):
-            return tile[:, m * N : (m + 1) * N]
+        identity = held.tile([P, P], F32, name="identity")
+        make_identity(nc, identity[:])
+        identity_bf = held.tile([P, P], BF16, name="identity_bf")
+        nc.vector.tensor_copy(identity_bf[:], identity[:])
+
+        blocks_of_ones = held.tile([P, P], F32, name="blocks_of_ones")
+        make_block_diagonal(nc, blocks_of_ones[:], CARD)
+        group_sum = held.tile([P, GROUPS], F32, name="group_sum")
+        nc.vector.tensor_copy(
+            group_sum[:], blocks_of_ones[:].rearrange("p (g t) -> p g t", t=CARD)[:, :, 0]
+        )
+        group_diff = held.tile([P, GROUPS], F32, name="group_diff")
+        nc.vector.tensor_scalar_mul(group_diff[:], group_sum[:], -1.0)
 
         neg_mu = held.tile([P, M * N], F32, name="neg_mu")
-        nc.vector.tensor_scalar_mul(neg_mu[:], mu[:], -1.0)
+        for m in range(M):
+            nc.vector.tensor_scalar_mul(neg_mu[:, m * N : (m + 1) * N], mu[:, m * N : (m + 1) * N], -1.0)
 
-        inv_sd = held.tile([P, M * N], F32, name="inv_sd")
-        nc.vector.reciprocal(inv_sd[:], sd[:])
+        cols_ps = flipped.tile([P, PIECE], F32, name="cols_ps", tag="diff_t")
+        nc.tensor.transpose(cols_ps[:, 0:P], rows[:], identity[:])
+        cols = held.tile([P, P], F32, name="cols")
+        nc.vector.tensor_copy(cols[:], cols_ps[:, 0:P])
+        sd = cols[:, 0 : M * COLS]
+        w = cols[:, 32 : 32 + M * COLS]
 
-        wmax = held.tile([P, N], F32, name="wmax")
-        nc.vector.tensor_max(wmax[:], leaf(w, 0), leaf(w, 1))
-        nc.vector.tensor_max(wmax[:], wmax[:], leaf(w, 2))
-        nc.vector.tensor_tensor(by_leaf(w), by_leaf(w), for_all_leaves(wmax), ALU.subtract)
-        exp_w = held.tile([P, M * N], F32, name="exp_w")
-        nc.scalar.activation(exp_w[:], w[:], FUNC.Exp)
-        wsum = held.tile([P, N], F32, name="wsum")
-        nc.vector.tensor_add(wsum[:], leaf(exp_w, 0), leaf(exp_w, 1))
-        nc.vector.tensor_add(wsum[:], wsum[:], leaf(exp_w, 2))
-        log_wsum = held.tile([P, N], F32, name="log_wsum")
+        def by_leaf(ap):
+            return ap.rearrange("p (m b) -> p m b", m=M)
+
+        def for_all_leaves(ap):
+            return ap.unsqueeze(1).to_broadcast([P, M, COLS])
+
+        z_scale = held.tile([P, M * COLS], F32, name="z_scale")
+        nc.vector.reciprocal(z_scale[:], sd)
+        nc.vector.tensor_scalar_mul(z_scale[:], z_scale[:], math.sqrt(0.5))
+
+        wmax = held.tile([P, COLS], F32, name="wmax")
+        nc.vector.tensor_max(wmax[:], w[:, 0:COLS], w[:, COLS : 2 * COLS])
+        nc.vector.tensor_max(wmax[:], wmax[:], w[:, 2 * COLS : 3 * COLS])
+        k = held.tile([P, M * COLS], F32, name="k")
+        nc.vector.tensor_tensor(by_leaf(k[:]), by_leaf(w), for_all_leaves(wmax[:]), ALU.subtract)
+        exp_w = held.tile([P, M * COLS], F32, name="exp_w")
+        nc.scalar.activation(exp_w[:], k[:], FUNC.Exp)
+        wsum = held.tile([P, COLS], F32, name="wsum")
+        nc.vector.tensor_add(wsum[:], exp_w[:, 0:COLS], exp_w[:, COLS : 2 * COLS])
+        nc.vector.tensor_add(wsum[:], wsum[:], exp_w[:, 2 * COLS : 3 * COLS])
+        log_wsum = held.tile([P, COLS], F32, name="log_wsum")
         nc.scalar.activation(log_wsum[:], wsum[:], FUNC.Ln)
-        log_sd = held.tile([P, M * N], F32, name="log_sd")
-        nc.scalar.activation(log_sd[:], sd[:], FUNC.Ln)
-
-        k = held.tile([P, M * N], F32, name="k")
-        nc.vector.tensor_sub(k[:], w[:], log_sd[:])
+        log_sd = held.tile([P, M * COLS], F32, name="log_sd")
+        nc.scalar.activation(log_sd[:], sd, FUNC.Ln)
+        nc.vector.tensor_sub(k[:], k[:], log_sd[:])
         nc.vector.scalar_tensor_tensor(
-            by_leaf(k), by_leaf(k), HALF_LOG_2PI, for_all_leaves(log_wsum), ALU.subtract, ALU.subtract
+            by_leaf(k[:]), by_leaf(k[:]), HALF_LOG_2PI, for_all_leaves(log_wsum[:]), ALU.subtract, ALU.subtract
         )
 
-        for b in range(C // P):
-            term = work.tile([P, M * N], F32, name="term")
-            for m in range(M):
-                nc.vector.tensor_tensor(
-                    leaf(term, m), windows[b][:].indirect(offsets[:]), leaf(neg_mu, m), ALU.add
-                )
-            nc.vector.tensor_mul(term[:], term[:], inv_sd[:])
-            nc.scalar.activation(term[:], term[:], FUNC.Square, scale=math.sqrt(0.5))
-            nc.vector.tensor_sub(term[:], k[:], term[:])
+        def square(s):
+            return slice(s * P, (s + 1) * P)
 
-            top = work.tile([P, N], F32, name="top")
-            nc.vector.tensor_max(top[:], leaf(term, 0), leaf(term, 1))
-            nc.vector.tensor_max(top[:], top[:], leaf(term, 2))
-            nc.vector.tensor_tensor(by_leaf(term), by_leaf(term), for_all_leaves(top), ALU.subtract)
-            nc.scalar.activation(term[:], term[:], FUNC.Exp)
+        def column(tile, m, piece, s):
+            c = m * COLS + piece * SUBS + s
+            return tile[:, c : c + 1]
 
-            mix = work.tile([P, N], F32, name="mix")
-            nc.vector.tensor_add(mix[:], leaf(term, 0), leaf(term, 1))
-            nc.vector.tensor_add(mix[:], mix[:], leaf(term, 2))
-            nc.scalar.activation(mix[:], mix[:], FUNC.Ln)
-            nc.vector.tensor_add(mix[:], mix[:], top[:])
+        diffs = {}
+        halves = {}
+        lows = {}
+        weights = {}
+        mixes = {}
 
-            product = work.tile([P, N // CARD], F32, name="product")
-            nc.vector.reduce_sum(
-                product[:], mix[:].rearrange("p (q t) -> p q t", t=CARD), axis=mybir.AxisListType.X
+        def look_up(chunk, m):
+            b, piece = divmod(chunk, PIECES)
+            if m == 0:
+                diffs[chunk] = short.tile([P, M, PIECE], F32, name="diff")
+            nc.vector.tensor_tensor(
+                diffs[chunk][:, m, :],
+                windows[b][:].indirect(offsets[:, piece * (PIECE // 16) : (piece + 1) * (PIECE // 16)]),
+                neg_mu[:, m * N + piece * PIECE : m * N + (piece + 1) * PIECE],
+                ALU.add,
             )
-            nc.sync.dma_start(out[b * P : (b + 1) * P, :], product[:])
+
+        def flip_and_square(chunk, m):
+            piece = chunk % PIECES
+            if m == 0:
+                halves[chunk] = long.tile([P, M, PIECE], F32, name="half")
+            diff_t = flipped.tile([P, PIECE], F32, name="diff_t")
+            for s in range(SUBS):
+                nc.tensor.transpose(diff_t[:, square(s)], diffs[chunk][:, m, square(s)], identity[:])
+            for s in range(SUBS):
+                nc.scalar.activation(
+                    halves[chunk][:, m, square(s)], diff_t[:, square(s)], FUNC.Square,
+                    scale=column(z_scale, m, piece, s),
+                )
+
+        def smallest(chunk):
+            piece = chunk % PIECES
+            half = halves[chunk]
+            umin = kept.tile([P, PIECE], F32, name="umin")
+            for s in range(SUBS):
+                nc.vector.tensor_scalar_sub(umin[:, square(s)], half[:, 2, square(s)], column(k, 2, piece, s))
+                for m in (1, 0):
+                    nc.vector.scalar_tensor_tensor(
+                        umin[:, square(s)], half[:, m, square(s)], column(k, m, piece, s), umin[:, square(s)],
+                        ALU.subtract, ALU.min,
+                    )
+            for m in range(M):
+                nc.gpsimd.tensor_tensor(half[:, m, :], half[:, m, :], umin[:], ALU.subtract)
+            lows[chunk] = umin
+
+        def weigh(chunk, m):
+            piece = chunk % PIECES
+            if m == 0:
+                weights[chunk] = short.tile([P, M, PIECE], BF16, name="weight")
+            for s in range(SUBS):
+                nc.scalar.activation(
+                    weights[chunk][:, m, square(s)], halves[chunk][:, m, square(s)], FUNC.Exp,
+                    bias=column(k, m, piece, s), scale=-1.0,
+                )
+
+        def add_up(chunk):
+            total = sums.tile([P, PIECE], F32, name="total")
+            for m in range(M):
+                nc.tensor.matmul(total[:], identity_bf[:], weights[chunk][:, m, :], start=(m == 0), stop=(m == M - 1))
+            mixes[chunk] = total
+
+        def finish(first_chunk):
+            product_ps = products.tile([P, BATCH * SUBS * GROUPS], F32, name="product_ps")
+            for i in range(BATCH):
+                chunk = first_chunk + i
+                log_mix = short.tile([P, PIECE], F32, name="log_mix")
+                nc.scalar.activation(log_mix[:], mixes[chunk][:], FUNC.Ln)
+                for s in range(SUBS):
+                    g = (i * SUBS + s) * GROUPS
+                    nc.tensor.matmul(
+                        product_ps[:, g : g + GROUPS], log_mix[:, square(s)], group_sum[:], start=True, stop=False
+                    )
+                    nc.tensor.matmul(
+                        product_ps[:, g : g + GROUPS], lows[chunk][:, square(s)], group_diff[:], start=False, stop=True
+                    )
+            product = short.tile([P, BATCH * SUBS * GROUPS], F32, name="product")
+            nc.scalar.copy(product[:], product_ps[:])
+            width = N // CARD
+            for i in range(BATCH // PIECES):
+                b = first_chunk // PIECES + i
+                nc.sync.dma_start(out[b * P : (b + 1) * P, :], product[:, i * width : (i + 1) * width])
+
+        def is_chunk(chunk):
+            return 0 <= chunk < CHUNKS
+
+        for step in range(CHUNKS + 3):
+            if is_chunk(step - 3):
+                add_up(step - 3)
+                if (step - 3) % BATCH == BATCH - 1:
+                    finish(step - 3 - (BATCH - 1))
+            for m in range(M):
+                if is_chunk(step):
+                    look_up(step, m)
+                    flip_and_square(step, m)
+                if is_chunk(step - 2):
+                    weigh(step - 2, m)
+            if is_chunk(step - 1):
+                smallest(step - 1)

@@ -20,7 +20,8 @@ SUBS = PIECE // P
 COLS = N // P
 GROUPS = P // CARD
 CHUNKS = BLOCKS * PIECES
-BATCH = 2 * PIECES
+WIDTH = PIECE // CARD
+BANK = 512
 
 
 def tile_spnneuronbig_kernel(tc, x, means, stds, w1, offs, out):
@@ -28,36 +29,26 @@ def tile_spnneuronbig_kernel(tc, x, means, stds, w1, offs, out):
     with (
         tc.tile_pool(name="held", bufs=1) as held,
         tc.tile_pool(name="tables", bufs=BLOCKS) as tables,
-        tc.tile_pool(name="short", bufs=3) as short,
-        tc.tile_pool(name="long", bufs=5) as long,
-        tc.tile_pool(name="kept", bufs=CHUNKS) as kept,
+        tc.tile_pool(name="ring", bufs=4) as ring,
         tc.psum_pool(name="flipped", bufs=3) as flipped,
-        tc.psum_pool(name="sums", bufs=BATCH) as sums,
-        tc.psum_pool(name="products", bufs=1) as products,
+        tc.psum_pool(name="mixes", bufs=2) as mixes,
+        tc.psum_pool(name="low_sums", bufs=CHUNKS * WIDTH // BANK) as low_sums,
     ):
         offsets = held.tile([P, N // 16], U16, name="offsets")
         nc.sync.dma_start(offsets[:], offs)
+
+        windows = [tables.tile([P, S], F32, name="window") for b in range(BLOCKS)]
+        for b in range(BLOCKS):
+            nc.sync.dma_start(windows[b][:], x[b * P : (b + 1) * P, :])
+
+        mu = held.tile([P, M * N], F32, name="mu")
+        for m in range(M):
+            nc.scalar.dma_start(mu[:, m * N : (m + 1) * N], means[m, :].partition_broadcast(P))
 
         rows = held.tile([P, P], F32, name="rows")
         nc.vector.memset(rows[:], 1.0)
         nc.scalar.dma_start(rows[0 : M * COLS, :], stds.rearrange("m (b p) -> (m b) p", p=P))
         nc.scalar.dma_start(rows[32 : 32 + M * COLS, :], w1.rearrange("m (b p) -> (m b) p", p=P))
-
-        mu = held.tile([P, M * N], F32, name="mu")
-        windows = [tables.tile([P, S], F32, name="window") for b in range(BLOCKS)]
-
-        def load_means(m):
-            nc.sync.dma_start(mu[:, m * N : (m + 1) * N], means[m, :].partition_broadcast(P))
-
-        def load_block(b):
-            nc.sync.dma_start(windows[b][:], x[b * P : (b + 1) * P, :])
-
-        load_means(0)
-        load_block(0)
-        for m in range(1, M):
-            load_means(m)
-        for b in range(1, BLOCKS):
-            load_block(b)
 
         identity = held.tile([P, P], F32, name="identity")
         make_identity(nc, identity[:])
@@ -70,8 +61,6 @@ def tile_spnneuronbig_kernel(tc, x, means, stds, w1, offs, out):
         nc.vector.tensor_copy(
             group_sum[:], blocks_of_ones[:].rearrange("p (g t) -> p g t", t=CARD)[:, :, 0]
         )
-        group_diff = held.tile([P, GROUPS], F32, name="group_diff")
-        nc.vector.tensor_scalar_mul(group_diff[:], group_sum[:], -1.0)
 
         neg_mu = held.tile([P, M * N], F32, name="neg_mu")
         for m in range(M):
@@ -122,14 +111,14 @@ def tile_spnneuronbig_kernel(tc, x, means, stds, w1, offs, out):
 
         diffs = {}
         halves = {}
-        lows = {}
         weights = {}
-        mixes = {}
+        mix_products = held.tile([P, CHUNKS * WIDTH], F32, name="mix_products")
+        low_sum = [low_sums.tile([P, BANK], F32, name="low_sum") for i in range(CHUNKS * WIDTH // BANK)]
 
         def look_up(chunk, m):
             b, piece = divmod(chunk, PIECES)
             if m == 0:
-                diffs[chunk] = short.tile([P, M, PIECE], F32, name="diff")
+                diffs[chunk] = ring.tile([P, M, PIECE], F32, name="diff")
             nc.vector.tensor_tensor(
                 diffs[chunk][:, m, :],
                 windows[b][:].indirect(offsets[:, piece * (PIECE // 16) : (piece + 1) * (PIECE // 16)]),
@@ -140,7 +129,7 @@ def tile_spnneuronbig_kernel(tc, x, means, stds, w1, offs, out):
         def flip_and_square(chunk, m):
             piece = chunk % PIECES
             if m == 0:
-                halves[chunk] = long.tile([P, M, PIECE], F32, name="half")
+                halves[chunk] = ring.tile([P, M, PIECE], F32, name="half")
             diff_t = flipped.tile([P, PIECE], F32, name="diff_t")
             for s in range(SUBS):
                 nc.tensor.transpose(diff_t[:, square(s)], diffs[chunk][:, m, square(s)], identity[:])
@@ -153,7 +142,7 @@ def tile_spnneuronbig_kernel(tc, x, means, stds, w1, offs, out):
         def smallest(chunk):
             piece = chunk % PIECES
             half = halves[chunk]
-            umin = kept.tile([P, PIECE], F32, name="umin")
+            umin = ring.tile([P, PIECE], F32, name="umin")
             for s in range(SUBS):
                 nc.vector.tensor_scalar_sub(umin[:, square(s)], half[:, 2, square(s)], column(k, 2, piece, s))
                 for m in (1, 0):
@@ -161,55 +150,47 @@ def tile_spnneuronbig_kernel(tc, x, means, stds, w1, offs, out):
                         umin[:, square(s)], half[:, m, square(s)], column(k, m, piece, s), umin[:, square(s)],
                         ALU.subtract, ALU.min,
                     )
-            for m in range(M):
-                nc.gpsimd.tensor_tensor(half[:, m, :], half[:, m, :], umin[:], ALU.subtract)
-            lows[chunk] = umin
+            nc.vector.tensor_tensor(
+                half[:], half[:], umin[:].unsqueeze(1).to_broadcast([P, M, PIECE]), ALU.subtract
+            )
+            for s in range(SUBS):
+                g = chunk * WIDTH + s * GROUPS
+                nc.tensor.matmul(
+                    low_sum[g // BANK][:, g % BANK : g % BANK + GROUPS], umin[:, square(s)], group_sum[:],
+                    start=True, stop=True,
+                )
 
         def weigh(chunk, m):
             piece = chunk % PIECES
             if m == 0:
-                weights[chunk] = short.tile([P, M, PIECE], BF16, name="weight")
+                weights[chunk] = ring.tile([P, M, PIECE], BF16, name="weight")
             for s in range(SUBS):
                 nc.scalar.activation(
                     weights[chunk][:, m, square(s)], halves[chunk][:, m, square(s)], FUNC.Exp,
                     bias=column(k, m, piece, s), scale=-1.0,
                 )
 
-        def add_up(chunk):
-            total = sums.tile([P, PIECE], F32, name="total")
-            for m in range(M):
-                nc.tensor.matmul(total[:], identity_bf[:], weights[chunk][:, m, :], start=(m == 0), stop=(m == M - 1))
-            mixes[chunk] = total
-
-        def finish(first_chunk):
-            product_ps = products.tile([P, BATCH * SUBS * GROUPS], F32, name="product_ps")
-            for i in range(BATCH):
-                chunk = first_chunk + i
-                log_mix = short.tile([P, PIECE], F32, name="log_mix")
-                nc.scalar.activation(log_mix[:], mixes[chunk][:], FUNC.Ln)
-                for s in range(SUBS):
-                    g = (i * SUBS + s) * GROUPS
+        def mix(chunk):
+            mix_ps = mixes.tile([P, PIECE], F32, name="mix_ps")
+            for s in range(SUBS):
+                for m in range(M):
                     nc.tensor.matmul(
-                        product_ps[:, g : g + GROUPS], log_mix[:, square(s)], group_sum[:], start=True, stop=False
+                        mix_ps[:, square(s)], weights[chunk][:, m, square(s)], identity_bf[:],
+                        start=(m == 0), stop=(m == M - 1),
                     )
-                    nc.tensor.matmul(
-                        product_ps[:, g : g + GROUPS], lows[chunk][:, square(s)], group_diff[:], start=False, stop=True
-                    )
-            product = short.tile([P, BATCH * SUBS * GROUPS], F32, name="product")
-            nc.scalar.copy(product[:], product_ps[:])
-            width = N // CARD
-            for i in range(BATCH // PIECES):
-                b = first_chunk // PIECES + i
-                nc.sync.dma_start(out[b * P : (b + 1) * P, :], product[:, i * width : (i + 1) * width])
+            nc.vector.tensor_reduce(
+                mix_products[:, chunk * WIDTH : (chunk + 1) * WIDTH],
+                mix_ps[:].rearrange("p (g t) -> p g t", t=CARD),
+                mybir.AxisListType.X,
+                ALU.mult,
+            )
 
         def is_chunk(chunk):
             return 0 <= chunk < CHUNKS
 
         for step in range(CHUNKS + 3):
             if is_chunk(step - 3):
-                add_up(step - 3)
-                if (step - 3) % BATCH == BATCH - 1:
-                    finish(step - 3 - (BATCH - 1))
+                mix(step - 3)
             for m in range(M):
                 if is_chunk(step):
                     look_up(step, m)
@@ -218,3 +199,13 @@ def tile_spnneuronbig_kernel(tc, x, means, stds, w1, offs, out):
                     weigh(step - 2, m)
             if is_chunk(step - 1):
                 smallest(step - 1)
+
+        nc.scalar.activation(mix_products[:], mix_products[:], FUNC.Ln)
+        result = held.tile([P, CHUNKS * WIDTH], F32, name="result")
+        blocks_a_bank = BANK // (N // CARD)
+        for i in range(CHUNKS * WIDTH // BANK):
+            nc.vector.tensor_sub(result[:, i * BANK : (i + 1) * BANK], mix_products[:, i * BANK : (i + 1) * BANK], low_sum[i][:])
+            nc.sync.dma_start(
+                out[i * blocks_a_bank * P : (i + 1) * blocks_a_bank * P, :].rearrange("(b p) q -> p b q", p=P),
+                result[:, i * BANK : (i + 1) * BANK].rearrange("p (b q) -> p b q", b=blocks_a_bank),
+            )

@@ -34,21 +34,20 @@ def tile_spnneuronbig_kernel(tc, x, means, stds, w1, offs, out):
         tc.psum_pool(name="mixes", bufs=2) as mixes,
         tc.psum_pool(name="low_sums", bufs=CHUNKS * WIDTH // BANK) as low_sums,
     ):
+        rows = held.tile([P, P], F32, name="rows")
+        nc.gpsimd.memset(rows[:], 1.0)
+        for i, parameter in enumerate((stds, w1, means)):
+            nc.sync.dma_start(rows[32 * i : 32 * i + M * COLS, :], parameter.rearrange("m (b p) -> (m b) p", p=P))
+
         offsets = held.tile([P, N // 16], U16, name="offsets")
         nc.sync.dma_start(offsets[:], offs)
+
+        mu = held.tile([P, N], F32, name="mu")
+        nc.sync.dma_start(mu[:], means[0, :].partition_broadcast(P))
 
         windows = [tables.tile([P, S], F32, name="window") for b in range(BLOCKS)]
         for b in range(BLOCKS):
             nc.sync.dma_start(windows[b][:], x[b * P : (b + 1) * P, :])
-
-        mu = held.tile([P, M * N], F32, name="mu")
-        for m in range(M):
-            nc.scalar.dma_start(mu[:, m * N : (m + 1) * N], means[m, :].partition_broadcast(P))
-
-        rows = held.tile([P, P], F32, name="rows")
-        nc.vector.memset(rows[:], 1.0)
-        nc.scalar.dma_start(rows[0 : M * COLS, :], stds.rearrange("m (b p) -> (m b) p", p=P))
-        nc.scalar.dma_start(rows[32 : 32 + M * COLS, :], w1.rearrange("m (b p) -> (m b) p", p=P))
 
         identity = held.tile([P, P], F32, name="identity")
         make_identity(nc, identity[:])
@@ -62,9 +61,8 @@ def tile_spnneuronbig_kernel(tc, x, means, stds, w1, offs, out):
             group_sum[:], blocks_of_ones[:].rearrange("p (g t) -> p g t", t=CARD)[:, :, 0]
         )
 
-        neg_mu = held.tile([P, M * N], F32, name="neg_mu")
-        for m in range(M):
-            nc.vector.tensor_scalar_mul(neg_mu[:, m * N : (m + 1) * N], mu[:, m * N : (m + 1) * N], -1.0)
+        neg_mu = held.tile([P, N], F32, name="neg_mu")
+        nc.vector.tensor_scalar_mul(neg_mu[:], mu[:], -1.0)
 
         cols_ps = flipped.tile([P, PIECE], F32, name="cols_ps", tag="diff_t")
         nc.tensor.transpose(cols_ps[:, 0:P], rows[:], identity[:])
@@ -72,6 +70,7 @@ def tile_spnneuronbig_kernel(tc, x, means, stds, w1, offs, out):
         nc.vector.tensor_copy(cols[:], cols_ps[:, 0:P])
         sd = cols[:, 0 : M * COLS]
         w = cols[:, 32 : 32 + M * COLS]
+        mean = cols[:, 64 : 64 + M * COLS]
 
         def by_leaf(ap):
             return ap.rearrange("p (m b) -> p m b", m=M)
@@ -82,6 +81,9 @@ def tile_spnneuronbig_kernel(tc, x, means, stds, w1, offs, out):
         z_scale = held.tile([P, M * COLS], F32, name="z_scale")
         nc.vector.reciprocal(z_scale[:], sd)
         nc.vector.tensor_scalar_mul(z_scale[:], z_scale[:], math.sqrt(0.5))
+        z_shift = held.tile([P, M * COLS], F32, name="z_shift")
+        nc.vector.tensor_tensor(by_leaf(z_shift[:]), for_all_leaves(mean[:, 0:COLS]), by_leaf(mean), ALU.subtract)
+        nc.vector.tensor_mul(z_shift[:], z_shift[:], z_scale[:])
 
         wmax = held.tile([P, COLS], F32, name="wmax")
         nc.vector.tensor_max(wmax[:], w[:, 0:COLS], w[:, COLS : 2 * COLS])
@@ -115,28 +117,27 @@ def tile_spnneuronbig_kernel(tc, x, means, stds, w1, offs, out):
         mix_products = held.tile([P, CHUNKS * WIDTH], F32, name="mix_products")
         low_sum = [low_sums.tile([P, BANK], F32, name="low_sum") for i in range(CHUNKS * WIDTH // BANK)]
 
-        def look_up(chunk, m):
+        def look_up_and_flip(chunk):
             b, piece = divmod(chunk, PIECES)
-            if m == 0:
-                diffs[chunk] = ring.tile([P, M, PIECE], F32, name="diff")
+            diff = ring.tile([P, PIECE], F32, name="diff")
             nc.vector.tensor_tensor(
-                diffs[chunk][:, m, :],
+                diff[:],
                 windows[b][:].indirect(offsets[:, piece * (PIECE // 16) : (piece + 1) * (PIECE // 16)]),
-                neg_mu[:, m * N + piece * PIECE : m * N + (piece + 1) * PIECE],
+                neg_mu[:, piece * PIECE : (piece + 1) * PIECE],
                 ALU.add,
             )
-
-        def flip_and_square(chunk, m):
-            piece = chunk % PIECES
-            if m == 0:
-                halves[chunk] = ring.tile([P, M, PIECE], F32, name="half")
             diff_t = flipped.tile([P, PIECE], F32, name="diff_t")
             for s in range(SUBS):
-                nc.tensor.transpose(diff_t[:, square(s)], diffs[chunk][:, m, square(s)], identity[:])
+                nc.tensor.transpose(diff_t[:, square(s)], diff[:, square(s)], identity[:])
+            diffs[chunk] = diff_t
+            halves[chunk] = ring.tile([P, M, PIECE], F32, name="half")
+
+        def score(chunk, m):
+            piece = chunk % PIECES
             for s in range(SUBS):
                 nc.scalar.activation(
-                    halves[chunk][:, m, square(s)], diff_t[:, square(s)], FUNC.Square,
-                    scale=column(z_scale, m, piece, s),
+                    halves[chunk][:, m, square(s)], diffs[chunk][:, square(s)], FUNC.Square,
+                    bias=column(z_shift, m, piece, s), scale=column(z_scale, m, piece, s),
                 )
 
         def smallest(chunk):
@@ -191,10 +192,11 @@ def tile_spnneuronbig_kernel(tc, x, means, stds, w1, offs, out):
         for step in range(CHUNKS + 3):
             if is_chunk(step - 3):
                 mix(step - 3)
+            if is_chunk(step):
+                look_up_and_flip(step)
             for m in range(M):
                 if is_chunk(step):
-                    look_up(step, m)
-                    flip_and_square(step, m)
+                    score(step, m)
                 if is_chunk(step - 2):
                     weigh(step - 2, m)
             if is_chunk(step - 1):

@@ -29,9 +29,9 @@ def tile_spnneuronbig_kernel(tc, x, means, stds, w1, offs, out):
     with (
         tc.tile_pool(name="held", bufs=1) as held,
         tc.tile_pool(name="tables", bufs=BLOCKS) as tables,
-        tc.tile_pool(name="ring", bufs=4) as ring,
+        tc.tile_pool(name="ring", bufs=CHUNKS) as ring,
         tc.psum_pool(name="flipped", bufs=3) as flipped,
-        tc.psum_pool(name="mixes", bufs=2) as mixes,
+        tc.psum_pool(name="mixes", bufs=3) as mixes,
         tc.psum_pool(name="low_sums", bufs=CHUNKS * WIDTH // BANK) as low_sums,
     ):
         rows = held.tile([P, P], F32, name="rows")
@@ -95,14 +95,10 @@ def tile_spnneuronbig_kernel(tc, x, means, stds, w1, offs, out):
         wsum = held.tile([P, COLS], F32, name="wsum")
         nc.vector.tensor_add(wsum[:], exp_w[:, 0:COLS], exp_w[:, COLS : 2 * COLS])
         nc.vector.tensor_add(wsum[:], wsum[:], exp_w[:, 2 * COLS : 3 * COLS])
-        log_wsum = held.tile([P, COLS], F32, name="log_wsum")
-        nc.scalar.activation(log_wsum[:], wsum[:], FUNC.Ln)
-        log_sd = held.tile([P, M * COLS], F32, name="log_sd")
-        nc.scalar.activation(log_sd[:], sd, FUNC.Ln)
-        nc.vector.tensor_sub(k[:], k[:], log_sd[:])
-        nc.vector.scalar_tensor_tensor(
-            by_leaf(k[:]), by_leaf(k[:]), HALF_LOG_2PI, for_all_leaves(log_wsum[:]), ALU.subtract, ALU.subtract
-        )
+        log_norm = held.tile([P, M * COLS], F32, name="log_norm")
+        nc.vector.tensor_tensor(by_leaf(log_norm[:]), by_leaf(sd), for_all_leaves(wsum[:]), ALU.mult)
+        nc.scalar.activation(log_norm[:], log_norm[:], FUNC.Ln)
+        nc.vector.scalar_tensor_tensor(k[:], k[:], HALF_LOG_2PI, log_norm[:], ALU.subtract, ALU.subtract)
 
         def square(s):
             return slice(s * P, (s + 1) * P)
@@ -146,14 +142,14 @@ def tile_spnneuronbig_kernel(tc, x, means, stds, w1, offs, out):
             umin = ring.tile([P, PIECE], F32, name="umin")
             for s in range(SUBS):
                 nc.vector.tensor_scalar_sub(umin[:, square(s)], half[:, 2, square(s)], column(k, 2, piece, s))
-                for m in (1, 0):
+            for m in (1, 0):
+                for s in range(SUBS):
                     nc.vector.scalar_tensor_tensor(
                         umin[:, square(s)], half[:, m, square(s)], column(k, m, piece, s), umin[:, square(s)],
                         ALU.subtract, ALU.min,
                     )
-            nc.vector.tensor_tensor(
-                half[:], half[:], umin[:].unsqueeze(1).to_broadcast([P, M, PIECE]), ALU.subtract
-            )
+            for m in range(M):
+                nc.vector.tensor_sub(half[:, m, :], half[:, m, :], umin[:])
             for s in range(SUBS):
                 g = chunk * WIDTH + s * GROUPS
                 nc.tensor.matmul(
@@ -190,8 +186,6 @@ def tile_spnneuronbig_kernel(tc, x, means, stds, w1, offs, out):
             return 0 <= chunk < CHUNKS
 
         for step in range(CHUNKS + 3):
-            if is_chunk(step - 3):
-                mix(step - 3)
             if is_chunk(step):
                 look_up_and_flip(step)
             for m in range(M):
@@ -201,13 +195,15 @@ def tile_spnneuronbig_kernel(tc, x, means, stds, w1, offs, out):
                     weigh(step - 2, m)
             if is_chunk(step - 1):
                 smallest(step - 1)
+            if is_chunk(step - 3):
+                mix(step - 3)
 
         nc.scalar.activation(mix_products[:], mix_products[:], FUNC.Ln)
         result = held.tile([P, CHUNKS * WIDTH], F32, name="result")
         blocks_a_bank = BANK // (N // CARD)
         for i in range(CHUNKS * WIDTH // BANK):
             nc.vector.tensor_sub(result[:, i * BANK : (i + 1) * BANK], mix_products[:, i * BANK : (i + 1) * BANK], low_sum[i][:])
-            nc.sync.dma_start(
+            (nc.sync, nc.scalar)[i % 2].dma_start(
                 out[i * blocks_a_bank * P : (i + 1) * blocks_a_bank * P, :].rearrange("(b p) q -> p b q", p=P),
                 result[:, i * BANK : (i + 1) * BANK].rearrange("p (b q) -> p b q", b=blocks_a_bank),
             )

@@ -14,13 +14,15 @@ C, S, N, M, CARD = 512, 4096, 1024, 3, 4
 HALF_LOG_2PI = 0.5 * math.log(2.0 * math.pi)
 
 BLOCKS = C // P
-PIECE = 512
+SPAN = 2
+WIDE = SPAN * P
+PIECE = 256
 PIECES = N // PIECE
 SUBS = PIECE // P
 COLS = N // P
 GROUPS = P // CARD
-CHUNKS = BLOCKS * PIECES
-WIDTH = PIECE // CARD
+CHUNKS = (BLOCKS // SPAN) * PIECES
+PRODUCTS = N // CARD
 BANK = 512
 
 
@@ -30,9 +32,10 @@ def tile_spnneuronbig_kernel(tc, x, means, stds, w1, offs, out):
         tc.tile_pool(name="held", bufs=1) as held,
         tc.tile_pool(name="tables", bufs=BLOCKS) as tables,
         tc.tile_pool(name="ring", bufs=CHUNKS) as ring,
+        tc.tile_pool(name="looked_up", bufs=SPAN * CHUNKS) as looked_up,
         tc.psum_pool(name="flipped", bufs=3) as flipped,
         tc.psum_pool(name="mixes", bufs=3) as mixes,
-        tc.psum_pool(name="low_sums", bufs=CHUNKS * WIDTH // BANK) as low_sums,
+        tc.psum_pool(name="low_sums", bufs=BLOCKS * PRODUCTS // BANK) as low_sums,
     ):
         rows = held.tile([P, P], F32, name="rows")
         nc.gpsimd.memset(rows[:], 1.0)
@@ -64,7 +67,7 @@ def tile_spnneuronbig_kernel(tc, x, means, stds, w1, offs, out):
         neg_mu = held.tile([P, N], F32, name="neg_mu")
         nc.vector.tensor_scalar_mul(neg_mu[:], mu[:], -1.0)
 
-        cols_ps = flipped.tile([P, PIECE], F32, name="cols_ps", tag="diff_t")
+        cols_ps = flipped.tile([P, BANK], F32, name="cols_ps", tag="diff_t")
         nc.tensor.transpose(cols_ps[:, 0:P], rows[:], identity[:])
         cols = held.tile([P, P], F32, name="cols")
         nc.vector.tensor_copy(cols[:], cols_ps[:, 0:P])
@@ -110,74 +113,82 @@ def tile_spnneuronbig_kernel(tc, x, means, stds, w1, offs, out):
         diffs = {}
         halves = {}
         weights = {}
-        mix_products = held.tile([P, CHUNKS * WIDTH], F32, name="mix_products")
-        low_sum = [low_sums.tile([P, BANK], F32, name="low_sum") for i in range(CHUNKS * WIDTH // BANK)]
+        mix_products = held.tile([P, BLOCKS * PRODUCTS], F32, name="mix_products")
+        low_sum = [low_sums.tile([P, BANK], F32, name="low_sum") for i in range(BLOCKS * PRODUCTS // BANK)]
+
+        def block(i):
+            return slice(i * P, (i + 1) * P)
 
         def look_up_and_flip(chunk):
-            b, piece = divmod(chunk, PIECES)
-            diff = ring.tile([P, PIECE], F32, name="diff")
-            nc.vector.tensor_tensor(
-                diff[:],
-                windows[b][:].indirect(offsets[:, piece * (PIECE // 16) : (piece + 1) * (PIECE // 16)]),
-                neg_mu[:, piece * PIECE : (piece + 1) * PIECE],
-                ALU.add,
-            )
-            diff_t = flipped.tile([P, PIECE], F32, name="diff_t")
-            for s in range(SUBS):
-                nc.tensor.transpose(diff_t[:, square(s)], diff[:, square(s)], identity[:])
+            span, piece = divmod(chunk, PIECES)
+            diff_t = flipped.tile([P, SUBS, WIDE], F32, name="diff_t")
+            for i in range(SPAN):
+                diff = looked_up.tile([P, PIECE], F32, name="diff")
+                nc.vector.tensor_tensor(
+                    diff[:],
+                    windows[span * SPAN + i][:].indirect(offsets[:, piece * (PIECE // 16) : (piece + 1) * (PIECE // 16)]),
+                    neg_mu[:, piece * PIECE : (piece + 1) * PIECE],
+                    ALU.add,
+                )
+                for s in range(SUBS):
+                    nc.tensor.transpose(diff_t[:, s, block(i)], diff[:, square(s)], identity[:])
             diffs[chunk] = diff_t
-            halves[chunk] = ring.tile([P, M, PIECE], F32, name="half")
+            halves[chunk] = ring.tile([P, M, SUBS, WIDE], F32, name="half")
 
         def score(chunk, m):
             piece = chunk % PIECES
             for s in range(SUBS):
                 nc.scalar.activation(
-                    halves[chunk][:, m, square(s)], diffs[chunk][:, square(s)], FUNC.Square,
+                    halves[chunk][:, m, s, :], diffs[chunk][:, s, :], FUNC.Square,
                     bias=column(z_shift, m, piece, s), scale=column(z_scale, m, piece, s),
                 )
 
         def smallest(chunk):
-            piece = chunk % PIECES
+            span, piece = divmod(chunk, PIECES)
             half = halves[chunk]
-            umin = ring.tile([P, PIECE], F32, name="umin")
+            umin = ring.tile([P, SUBS, WIDE], F32, name="umin")
             for s in range(SUBS):
-                nc.vector.tensor_scalar_sub(umin[:, square(s)], half[:, 2, square(s)], column(k, 2, piece, s))
+                nc.vector.tensor_scalar_sub(umin[:, s, :], half[:, 2, s, :], column(k, 2, piece, s))
             for m in (1, 0):
                 for s in range(SUBS):
                     nc.vector.scalar_tensor_tensor(
-                        umin[:, square(s)], half[:, m, square(s)], column(k, m, piece, s), umin[:, square(s)],
-                        ALU.subtract, ALU.min,
+                        umin[:, s, :], half[:, m, s, :], column(k, m, piece, s), umin[:, s, :], ALU.subtract, ALU.min
                     )
             for m in range(M):
-                nc.vector.tensor_sub(half[:, m, :], half[:, m, :], umin[:])
-            for s in range(SUBS):
-                g = chunk * WIDTH + s * GROUPS
-                nc.tensor.matmul(
-                    low_sum[g // BANK][:, g % BANK : g % BANK + GROUPS], umin[:, square(s)], group_sum[:],
-                    start=True, stop=True,
-                )
+                nc.vector.tensor_sub(half[:, m, :, :], half[:, m, :, :], umin[:])
+            for i in range(SPAN):
+                for s in range(SUBS):
+                    g = (span * SPAN + i) * PRODUCTS + (piece * SUBS + s) * GROUPS
+                    nc.tensor.matmul(
+                        low_sum[g // BANK][:, g % BANK : g % BANK + GROUPS], umin[:, s, block(i)], group_sum[:],
+                        start=True, stop=True,
+                    )
 
         def weigh(chunk, m):
             piece = chunk % PIECES
             if m == 0:
-                weights[chunk] = ring.tile([P, M, PIECE], BF16, name="weight")
+                weights[chunk] = ring.tile([P, M, SUBS, WIDE], BF16, name="weight")
             for s in range(SUBS):
                 nc.scalar.activation(
-                    weights[chunk][:, m, square(s)], halves[chunk][:, m, square(s)], FUNC.Exp,
+                    weights[chunk][:, m, s, :], halves[chunk][:, m, s, :], FUNC.Exp,
                     bias=column(k, m, piece, s), scale=-1.0,
                 )
 
         def mix(chunk):
-            mix_ps = mixes.tile([P, PIECE], F32, name="mix_ps")
-            for s in range(SUBS):
-                for m in range(M):
-                    nc.tensor.matmul(
-                        mix_ps[:, square(s)], weights[chunk][:, m, square(s)], identity_bf[:],
-                        start=(m == 0), stop=(m == M - 1),
-                    )
+            span, piece = divmod(chunk, PIECES)
+            mix_ps = mixes.tile([P, SPAN, PIECE], F32, name="mix_ps")
+            for i in range(SPAN):
+                for s in range(SUBS):
+                    for m in range(M):
+                        nc.tensor.matmul(
+                            mix_ps[:, i, square(s)], weights[chunk][:, m, s, block(i)], identity_bf[:],
+                            start=(m == 0), stop=(m == M - 1),
+                        )
             nc.vector.tensor_reduce(
-                mix_products[:, chunk * WIDTH : (chunk + 1) * WIDTH],
-                mix_ps[:].rearrange("p (g t) -> p g t", t=CARD),
+                mix_products[:].rearrange("p (b q) -> p b q", b=BLOCKS)[
+                    :, span * SPAN : (span + 1) * SPAN, piece * (PIECE // CARD) : (piece + 1) * (PIECE // CARD)
+                ],
+                mix_ps[:].rearrange("p i (g t) -> p i g t", t=CARD),
                 mybir.AxisListType.X,
                 ALU.mult,
             )
@@ -186,6 +197,8 @@ def tile_spnneuronbig_kernel(tc, x, means, stds, w1, offs, out):
             return 0 <= chunk < CHUNKS
 
         for step in range(CHUNKS + 3):
+            if is_chunk(step - 3):
+                mix(step - 3)
             if is_chunk(step):
                 look_up_and_flip(step)
             for m in range(M):
@@ -195,13 +208,11 @@ def tile_spnneuronbig_kernel(tc, x, means, stds, w1, offs, out):
                     weigh(step - 2, m)
             if is_chunk(step - 1):
                 smallest(step - 1)
-            if is_chunk(step - 3):
-                mix(step - 3)
 
         nc.scalar.activation(mix_products[:], mix_products[:], FUNC.Ln)
-        result = held.tile([P, CHUNKS * WIDTH], F32, name="result")
-        blocks_a_bank = BANK // (N // CARD)
-        for i in range(CHUNKS * WIDTH // BANK):
+        result = held.tile([P, BLOCKS * PRODUCTS], F32, name="result")
+        blocks_a_bank = BANK // PRODUCTS
+        for i in range(BLOCKS * PRODUCTS // BANK):
             nc.vector.tensor_sub(result[:, i * BANK : (i + 1) * BANK], mix_products[:, i * BANK : (i + 1) * BANK], low_sum[i][:])
             (nc.sync, nc.scalar)[i % 2].dma_start(
                 out[i * blocks_a_bank * P : (i + 1) * blocks_a_bank * P, :].rearrange("(b p) q -> p b q", p=P),

@@ -14,15 +14,13 @@ C, S, N, M, CARD = 512, 4096, 1024, 3, 4
 HALF_LOG_2PI = 0.5 * math.log(2.0 * math.pi)
 
 BLOCKS = C // P
-SPAN = 2
-WIDE = SPAN * P
-PIECE = 256
+PIECE = 512
 PIECES = N // PIECE
 SUBS = PIECE // P
 COLS = N // P
 GROUPS = P // CARD
-CHUNKS = (BLOCKS // SPAN) * PIECES
-PRODUCTS = N // CARD
+CHUNKS = BLOCKS * PIECES
+WIDTH = PIECE // CARD
 BANK = 512
 
 
@@ -31,26 +29,35 @@ def tile_spnneuronbig_kernel(tc, x, means, stds, w1, offs, out):
     with (
         tc.tile_pool(name="held", bufs=1) as held,
         tc.tile_pool(name="tables", bufs=BLOCKS) as tables,
+        tc.tile_pool(name="short", bufs=4) as short,
         tc.tile_pool(name="ring", bufs=CHUNKS) as ring,
-        tc.tile_pool(name="looked_up", bufs=SPAN * CHUNKS) as looked_up,
         tc.psum_pool(name="flipped", bufs=3) as flipped,
         tc.psum_pool(name="mixes", bufs=3) as mixes,
-        tc.psum_pool(name="low_sums", bufs=BLOCKS * PRODUCTS // BANK) as low_sums,
+        tc.psum_pool(name="low_sums", bufs=CHUNKS * WIDTH // BANK) as low_sums,
     ):
         rows = held.tile([P, P], F32, name="rows")
         nc.gpsimd.memset(rows[:], 1.0)
-        for i, parameter in enumerate((stds, w1, means)):
+        for i, parameter in enumerate((stds, w1)):
             nc.sync.dma_start(rows[32 * i : 32 * i + M * COLS, :], parameter.rearrange("m (b p) -> (m b) p", p=P))
 
         offsets = held.tile([P, N // 16], U16, name="offsets")
         nc.sync.dma_start(offsets[:], offs)
 
-        mu = held.tile([P, N], F32, name="mu")
-        nc.sync.dma_start(mu[:], means[0, :].partition_broadcast(P))
-
+        mu = held.tile([P, M * N], F32, name="mu")
         windows = [tables.tile([P, S], F32, name="window") for b in range(BLOCKS)]
-        for b in range(BLOCKS):
+
+        def load_means(m):
+            nc.sync.dma_start(mu[:, m * N : (m + 1) * N], means[m, :].partition_broadcast(P))
+
+        def load_block(b):
             nc.sync.dma_start(windows[b][:], x[b * P : (b + 1) * P, :])
+
+        load_means(0)
+        load_block(0)
+        for m in range(1, M):
+            load_means(m)
+        for b in range(1, BLOCKS):
+            load_block(b)
 
         identity = held.tile([P, P], F32, name="identity")
         make_identity(nc, identity[:])
@@ -64,16 +71,16 @@ def tile_spnneuronbig_kernel(tc, x, means, stds, w1, offs, out):
             group_sum[:], blocks_of_ones[:].rearrange("p (g t) -> p g t", t=CARD)[:, :, 0]
         )
 
-        neg_mu = held.tile([P, N], F32, name="neg_mu")
-        nc.vector.tensor_scalar_mul(neg_mu[:], mu[:], -1.0)
+        neg_mu = held.tile([P, M * N], F32, name="neg_mu")
+        for m in range(M):
+            nc.vector.tensor_scalar_mul(neg_mu[:, m * N : (m + 1) * N], mu[:, m * N : (m + 1) * N], -1.0)
 
-        cols_ps = flipped.tile([P, BANK], F32, name="cols_ps", tag="diff_t")
+        cols_ps = flipped.tile([P, PIECE], F32, name="cols_ps", tag="diff_t")
         nc.tensor.transpose(cols_ps[:, 0:P], rows[:], identity[:])
         cols = held.tile([P, P], F32, name="cols")
         nc.vector.tensor_copy(cols[:], cols_ps[:, 0:P])
         sd = cols[:, 0 : M * COLS]
         w = cols[:, 32 : 32 + M * COLS]
-        mean = cols[:, 64 : 64 + M * COLS]
 
         def by_leaf(ap):
             return ap.rearrange("p (m b) -> p m b", m=M)
@@ -84,9 +91,6 @@ def tile_spnneuronbig_kernel(tc, x, means, stds, w1, offs, out):
         z_scale = held.tile([P, M * COLS], F32, name="z_scale")
         nc.vector.reciprocal(z_scale[:], sd)
         nc.vector.tensor_scalar_mul(z_scale[:], z_scale[:], math.sqrt(0.5))
-        z_shift = held.tile([P, M * COLS], F32, name="z_shift")
-        nc.vector.tensor_tensor(by_leaf(z_shift[:]), for_all_leaves(mean[:, 0:COLS]), by_leaf(mean), ALU.subtract)
-        nc.vector.tensor_mul(z_shift[:], z_shift[:], z_scale[:])
 
         wmax = held.tile([P, COLS], F32, name="wmax")
         nc.vector.tensor_max(wmax[:], w[:, 0:COLS], w[:, COLS : 2 * COLS])
@@ -113,82 +117,75 @@ def tile_spnneuronbig_kernel(tc, x, means, stds, w1, offs, out):
         diffs = {}
         halves = {}
         weights = {}
-        mix_products = held.tile([P, BLOCKS * PRODUCTS], F32, name="mix_products")
-        low_sum = [low_sums.tile([P, BANK], F32, name="low_sum") for i in range(BLOCKS * PRODUCTS // BANK)]
+        mix_products = held.tile([P, CHUNKS * WIDTH], F32, name="mix_products")
+        low_sum = [low_sums.tile([P, BANK], F32, name="low_sum") for i in range(CHUNKS * WIDTH // BANK)]
 
-        def block(i):
-            return slice(i * P, (i + 1) * P)
+        def look_up(chunk, m):
+            b, piece = divmod(chunk, PIECES)
+            if m == 0:
+                diffs[chunk] = short.tile([P, M, PIECE], F32, name="diff")
+            nc.vector.tensor_tensor(
+                diffs[chunk][:, m, :],
+                windows[b][:].indirect(offsets[:, piece * (PIECE // 16) : (piece + 1) * (PIECE // 16)]),
+                neg_mu[:, m * N + piece * PIECE : m * N + (piece + 1) * PIECE],
+                ALU.add,
+            )
 
-        def look_up_and_flip(chunk):
-            span, piece = divmod(chunk, PIECES)
-            diff_t = flipped.tile([P, SUBS, WIDE], F32, name="diff_t")
-            for i in range(SPAN):
-                diff = looked_up.tile([P, PIECE], F32, name="diff")
-                nc.vector.tensor_tensor(
-                    diff[:],
-                    windows[span * SPAN + i][:].indirect(offsets[:, piece * (PIECE // 16) : (piece + 1) * (PIECE // 16)]),
-                    neg_mu[:, piece * PIECE : (piece + 1) * PIECE],
-                    ALU.add,
-                )
-                for s in range(SUBS):
-                    nc.tensor.transpose(diff_t[:, s, block(i)], diff[:, square(s)], identity[:])
-            diffs[chunk] = diff_t
-            halves[chunk] = ring.tile([P, M, SUBS, WIDE], F32, name="half")
-
-        def score(chunk, m):
+        def flip_and_square(chunk, m):
             piece = chunk % PIECES
+            if m == 0:
+                halves[chunk] = ring.tile([P, M, PIECE], F32, name="half")
+            diff_t = flipped.tile([P, PIECE], F32, name="diff_t")
+            for s in range(SUBS):
+                nc.tensor.transpose(diff_t[:, square(s)], diffs[chunk][:, m, square(s)], identity[:])
             for s in range(SUBS):
                 nc.scalar.activation(
-                    halves[chunk][:, m, s, :], diffs[chunk][:, s, :], FUNC.Square,
-                    bias=column(z_shift, m, piece, s), scale=column(z_scale, m, piece, s),
+                    halves[chunk][:, m, square(s)], diff_t[:, square(s)], FUNC.Square,
+                    scale=column(z_scale, m, piece, s),
                 )
 
         def smallest(chunk):
-            span, piece = divmod(chunk, PIECES)
+            piece = chunk % PIECES
             half = halves[chunk]
-            umin = ring.tile([P, SUBS, WIDE], F32, name="umin")
+            umin = ring.tile([P, PIECE], F32, name="umin")
             for s in range(SUBS):
-                nc.vector.tensor_scalar_sub(umin[:, s, :], half[:, 2, s, :], column(k, 2, piece, s))
+                nc.vector.tensor_scalar_sub(umin[:, square(s)], half[:, 2, square(s)], column(k, 2, piece, s))
             for m in (1, 0):
                 for s in range(SUBS):
                     nc.vector.scalar_tensor_tensor(
-                        umin[:, s, :], half[:, m, s, :], column(k, m, piece, s), umin[:, s, :], ALU.subtract, ALU.min
+                        umin[:, square(s)], half[:, m, square(s)], column(k, m, piece, s), umin[:, square(s)],
+                        ALU.subtract, ALU.min,
                     )
             for m in range(M):
-                nc.vector.tensor_sub(half[:, m, :, :], half[:, m, :, :], umin[:])
-            for i in range(SPAN):
-                for s in range(SUBS):
-                    g = (span * SPAN + i) * PRODUCTS + (piece * SUBS + s) * GROUPS
-                    nc.tensor.matmul(
-                        low_sum[g // BANK][:, g % BANK : g % BANK + GROUPS], umin[:, s, block(i)], group_sum[:],
-                        start=True, stop=True,
-                    )
+                nc.vector.tensor_sub(half[:, m, :], half[:, m, :], umin[:])
+            for s in range(SUBS):
+                g = chunk * WIDTH + s * GROUPS
+                nc.tensor.matmul(
+                    low_sum[g // BANK][:, g % BANK : g % BANK + GROUPS], umin[:, square(s)], group_sum[:],
+                    start=True, stop=True,
+                )
 
         def weigh(chunk, m):
             piece = chunk % PIECES
             if m == 0:
-                weights[chunk] = ring.tile([P, M, SUBS, WIDE], BF16, name="weight")
+                weights[chunk] = ring.tile([P, M, PIECE], BF16, name="weight")
             for s in range(SUBS):
                 nc.scalar.activation(
-                    weights[chunk][:, m, s, :], halves[chunk][:, m, s, :], FUNC.Exp,
+                    weights[chunk][:, m, square(s)], halves[chunk][:, m, square(s)], FUNC.Exp,
                     bias=column(k, m, piece, s), scale=-1.0,
                 )
 
         def mix(chunk):
-            span, piece = divmod(chunk, PIECES)
-            mix_ps = mixes.tile([P, SPAN, PIECE], F32, name="mix_ps")
-            for i in range(SPAN):
-                for s in range(SUBS):
-                    for m in range(M):
-                        nc.tensor.matmul(
-                            mix_ps[:, i, square(s)], weights[chunk][:, m, s, block(i)], identity_bf[:],
-                            start=(m == 0), stop=(m == M - 1),
-                        )
+            mix_ps = mixes.tile([P, PIECE], F32, name="mix_ps")
+            for s in range(SUBS):
+                for m in range(M):
+                    nc.tensor.matmul(
+                        mix_ps[:, square(s)], weights[chunk][:, m, square(s)], identity_bf[:],
+                        start=(m == 0), stop=(m == M - 1),
+                    )
             nc.vector.tensor_reduce(
-                mix_products[:].rearrange("p (b q) -> p b q", b=BLOCKS)[
-                    :, span * SPAN : (span + 1) * SPAN, piece * (PIECE // CARD) : (piece + 1) * (PIECE // CARD)
-                ],
-                mix_ps[:].rearrange("p i (g t) -> p i g t", t=CARD),
+                mix_products[:, chunk * WIDTH : (chunk + 1) * WIDTH],
+                mix_ps[:].rearrange("p (g t) -> p g t", t=CARD),
                 mybir.AxisListType.X,
                 ALU.mult,
             )
@@ -199,20 +196,19 @@ def tile_spnneuronbig_kernel(tc, x, means, stds, w1, offs, out):
         for step in range(CHUNKS + 3):
             if is_chunk(step - 3):
                 mix(step - 3)
-            if is_chunk(step):
-                look_up_and_flip(step)
             for m in range(M):
                 if is_chunk(step):
-                    score(step, m)
+                    look_up(step, m)
+                    flip_and_square(step, m)
                 if is_chunk(step - 2):
                     weigh(step - 2, m)
             if is_chunk(step - 1):
                 smallest(step - 1)
 
         nc.scalar.activation(mix_products[:], mix_products[:], FUNC.Ln)
-        result = held.tile([P, BLOCKS * PRODUCTS], F32, name="result")
-        blocks_a_bank = BANK // PRODUCTS
-        for i in range(BLOCKS * PRODUCTS // BANK):
+        result = held.tile([P, CHUNKS * WIDTH], F32, name="result")
+        blocks_a_bank = BANK // (N // CARD)
+        for i in range(CHUNKS * WIDTH // BANK):
             nc.vector.tensor_sub(result[:, i * BANK : (i + 1) * BANK], mix_products[:, i * BANK : (i + 1) * BANK], low_sum[i][:])
             (nc.sync, nc.scalar)[i % 2].dma_start(
                 out[i * blocks_a_bank * P : (i + 1) * blocks_a_bank * P, :].rearrange("(b p) q -> p b q", p=P),

@@ -13,15 +13,17 @@ P = 128
 C, S, N, M, CARD = 512, 4096, 1024, 3, 4
 HALF_LOG_2PI = 0.5 * math.log(2.0 * math.pi)
 
+BANK = 512
 BLOCKS = C // P
-PIECE = 512
+PIECE = BANK
 PIECES = N // PIECE
 SUBS = PIECE // P
 COLS = N // P
+ROWS = M * COLS
 GROUPS = P // CARD
 CHUNKS = BLOCKS * PIECES
 WIDTH = PIECE // CARD
-BANK = 512
+RESULT_BANKS = CHUNKS * WIDTH // BANK
 
 
 def tile_spnneuronbig_kernel(tc, x, means, stds, w1, offs, out):
@@ -29,33 +31,32 @@ def tile_spnneuronbig_kernel(tc, x, means, stds, w1, offs, out):
     with (
         tc.tile_pool(name="held", bufs=1) as held,
         tc.tile_pool(name="tables", bufs=BLOCKS) as tables,
-        tc.tile_pool(name="short", bufs=4) as short,
         tc.tile_pool(name="ring", bufs=CHUNKS) as ring,
         tc.psum_pool(name="flipped", bufs=3) as flipped,
         tc.psum_pool(name="mixes", bufs=3) as mixes,
-        tc.psum_pool(name="low_sums", bufs=CHUNKS * WIDTH // BANK) as low_sums,
+        tc.psum_pool(name="low_sums", bufs=RESULT_BANKS) as low_sums,
     ):
-        rows = held.tile([P, P], F32, name="rows")
-        nc.gpsimd.memset(rows[:], 1.0)
-        for i, parameter in enumerate((stds, w1)):
-            nc.sync.dma_start(rows[32 * i : 32 * i + M * COLS, :], parameter.rearrange("m (b p) -> (m b) p", p=P))
+        rows = held.tile([3 * ROWS, P], F32, name="rows")
+        for i, parameter in enumerate((stds, w1, means)):
+            nc.sync.dma_start(rows[i * ROWS : (i + 1) * ROWS, :], parameter.rearrange("m (b p) -> (m b) p", p=P))
 
         offsets = held.tile([P, N // 16], U16, name="offsets")
         nc.sync.dma_start(offsets[:], offs)
 
-        mu = held.tile([P, M * N], F32, name="mu")
+        mu = held.tile([P, N], F32, name="mu")
         windows = [tables.tile([P, S], F32, name="window") for b in range(BLOCKS)]
 
-        def load_means(m):
-            nc.sync.dma_start(mu[:, m * N : (m + 1) * N], means[m, :].partition_broadcast(P))
+        def load_means(piece):
+            entries = slice(piece * PIECE, (piece + 1) * PIECE)
+            nc.sync.dma_start(mu[:, entries], means[0, entries].partition_broadcast(P))
 
         def load_block(b):
             nc.sync.dma_start(windows[b][:], x[b * P : (b + 1) * P, :])
 
         load_means(0)
         load_block(0)
-        for m in range(1, M):
-            load_means(m)
+        for piece in range(1, PIECES):
+            load_means(piece)
         for b in range(1, BLOCKS):
             load_block(b)
 
@@ -71,16 +72,18 @@ def tile_spnneuronbig_kernel(tc, x, means, stds, w1, offs, out):
             group_sum[:], blocks_of_ones[:].rearrange("p (g t) -> p g t", t=CARD)[:, :, 0]
         )
 
-        neg_mu = held.tile([P, M * N], F32, name="neg_mu")
-        for m in range(M):
-            nc.vector.tensor_scalar_mul(neg_mu[:, m * N : (m + 1) * N], mu[:, m * N : (m + 1) * N], -1.0)
+        neg_mu = held.tile([P, N], F32, name="neg_mu")
+        for piece in range(PIECES):
+            entries = slice(piece * PIECE, (piece + 1) * PIECE)
+            nc.vector.tensor_scalar_mul(neg_mu[:, entries], mu[:, entries], -1.0)
 
         cols_ps = flipped.tile([P, PIECE], F32, name="cols_ps", tag="diff_t")
-        nc.tensor.transpose(cols_ps[:, 0:P], rows[:], identity[:])
-        cols = held.tile([P, P], F32, name="cols")
-        nc.vector.tensor_copy(cols[:], cols_ps[:, 0:P])
-        sd = cols[:, 0 : M * COLS]
-        w = cols[:, 32 : 32 + M * COLS]
+        nc.tensor.transpose(cols_ps[:, 0 : 3 * ROWS], rows[:], identity[0 : 3 * ROWS, 0 : 3 * ROWS])
+        cols = held.tile([P, 3 * ROWS], F32, name="cols")
+        nc.vector.tensor_copy(cols[:], cols_ps[:, 0 : 3 * ROWS])
+        sd = cols[:, 0:ROWS]
+        w = cols[:, ROWS : 2 * ROWS]
+        mean = cols[:, 2 * ROWS : 3 * ROWS]
 
         def by_leaf(ap):
             return ap.rearrange("p (m b) -> p m b", m=M)
@@ -91,6 +94,9 @@ def tile_spnneuronbig_kernel(tc, x, means, stds, w1, offs, out):
         z_scale = held.tile([P, M * COLS], F32, name="z_scale")
         nc.vector.reciprocal(z_scale[:], sd)
         nc.vector.tensor_scalar_mul(z_scale[:], z_scale[:], math.sqrt(0.5))
+        z_shift = held.tile([P, M * COLS], F32, name="z_shift")
+        nc.vector.tensor_tensor(by_leaf(z_shift[:]), for_all_leaves(mean[:, 0:COLS]), by_leaf(mean), ALU.subtract)
+        nc.vector.tensor_mul(z_shift[:], z_shift[:], z_scale[:])
 
         wmax = held.tile([P, COLS], F32, name="wmax")
         nc.vector.tensor_max(wmax[:], w[:, 0:COLS], w[:, COLS : 2 * COLS])
@@ -102,10 +108,14 @@ def tile_spnneuronbig_kernel(tc, x, means, stds, w1, offs, out):
         wsum = held.tile([P, COLS], F32, name="wsum")
         nc.vector.tensor_add(wsum[:], exp_w[:, 0:COLS], exp_w[:, COLS : 2 * COLS])
         nc.vector.tensor_add(wsum[:], wsum[:], exp_w[:, 2 * COLS : 3 * COLS])
-        log_norm = held.tile([P, M * COLS], F32, name="log_norm")
-        nc.vector.tensor_tensor(by_leaf(log_norm[:]), by_leaf(sd), for_all_leaves(wsum[:]), ALU.mult)
-        nc.scalar.activation(log_norm[:], log_norm[:], FUNC.Ln)
-        nc.vector.scalar_tensor_tensor(k[:], k[:], HALF_LOG_2PI, log_norm[:], ALU.subtract, ALU.subtract)
+        log_wsum = held.tile([P, COLS], F32, name="log_wsum")
+        nc.scalar.activation(log_wsum[:], wsum[:], FUNC.Ln)
+        log_sd = held.tile([P, M * COLS], F32, name="log_sd")
+        nc.scalar.activation(log_sd[:], sd, FUNC.Ln)
+        nc.vector.tensor_sub(k[:], k[:], log_sd[:])
+        nc.vector.scalar_tensor_tensor(
+            by_leaf(k[:]), by_leaf(k[:]), HALF_LOG_2PI, for_all_leaves(log_wsum[:]), ALU.subtract, ALU.subtract
+        )
 
         def square(s):
             return slice(s * P, (s + 1) * P)
@@ -118,30 +128,29 @@ def tile_spnneuronbig_kernel(tc, x, means, stds, w1, offs, out):
         halves = {}
         weights = {}
         mix_products = held.tile([P, CHUNKS * WIDTH], F32, name="mix_products")
-        low_sum = [low_sums.tile([P, BANK], F32, name="low_sum") for i in range(CHUNKS * WIDTH // BANK)]
+        low_sum = [low_sums.tile([P, BANK], F32, name="low_sum") for i in range(RESULT_BANKS)]
 
-        def look_up(chunk, m):
+        def look_up_and_flip(chunk):
             b, piece = divmod(chunk, PIECES)
-            if m == 0:
-                diffs[chunk] = short.tile([P, M, PIECE], F32, name="diff")
+            diff = ring.tile([P, PIECE], F32, name="diff")
             nc.vector.tensor_tensor(
-                diffs[chunk][:, m, :],
+                diff[:],
                 windows[b][:].indirect(offsets[:, piece * (PIECE // 16) : (piece + 1) * (PIECE // 16)]),
-                neg_mu[:, m * N + piece * PIECE : m * N + (piece + 1) * PIECE],
+                neg_mu[:, piece * PIECE : (piece + 1) * PIECE],
                 ALU.add,
             )
-
-        def flip_and_square(chunk, m):
-            piece = chunk % PIECES
-            if m == 0:
-                halves[chunk] = ring.tile([P, M, PIECE], F32, name="half")
             diff_t = flipped.tile([P, PIECE], F32, name="diff_t")
             for s in range(SUBS):
-                nc.tensor.transpose(diff_t[:, square(s)], diffs[chunk][:, m, square(s)], identity[:])
+                nc.tensor.transpose(diff_t[:, square(s)], diff[:, square(s)], identity[:])
+            diffs[chunk] = diff_t
+            halves[chunk] = ring.tile([P, M, PIECE], F32, name="half")
+
+        def score(chunk, m):
+            piece = chunk % PIECES
             for s in range(SUBS):
                 nc.scalar.activation(
-                    halves[chunk][:, m, square(s)], diff_t[:, square(s)], FUNC.Square,
-                    scale=column(z_scale, m, piece, s),
+                    halves[chunk][:, m, square(s)], diffs[chunk][:, square(s)], FUNC.Square,
+                    bias=column(z_shift, m, piece, s), scale=column(z_scale, m, piece, s),
                 )
 
         def smallest(chunk):
@@ -196,10 +205,11 @@ def tile_spnneuronbig_kernel(tc, x, means, stds, w1, offs, out):
         for step in range(CHUNKS + 3):
             if is_chunk(step - 3):
                 mix(step - 3)
+            if is_chunk(step):
+                look_up_and_flip(step)
             for m in range(M):
                 if is_chunk(step):
-                    look_up(step, m)
-                    flip_and_square(step, m)
+                    score(step, m)
                 if is_chunk(step - 2):
                     weigh(step - 2, m)
             if is_chunk(step - 1):
@@ -208,9 +218,9 @@ def tile_spnneuronbig_kernel(tc, x, means, stds, w1, offs, out):
         nc.scalar.activation(mix_products[:], mix_products[:], FUNC.Ln)
         result = held.tile([P, CHUNKS * WIDTH], F32, name="result")
         blocks_a_bank = BANK // (N // CARD)
-        for i in range(CHUNKS * WIDTH // BANK):
+        for i in range(RESULT_BANKS):
             nc.vector.tensor_sub(result[:, i * BANK : (i + 1) * BANK], mix_products[:, i * BANK : (i + 1) * BANK], low_sum[i][:])
-            (nc.sync, nc.scalar)[i % 2].dma_start(
+            nc.sync.dma_start(
                 out[i * blocks_a_bank * P : (i + 1) * blocks_a_bank * P, :].rearrange("(b p) q -> p b q", p=P),
                 result[:, i * BANK : (i + 1) * BANK].rearrange("p (b q) -> p b q", b=blocks_a_bank),
             )

@@ -71,6 +71,10 @@ def tile_spnneuronbig_kernel(tc, x, means, stds, w1, offs, out):
         nc.vector.tensor_copy(
             group_sum[:], blocks_of_ones[:].rearrange("p (g t) -> p g t", t=CARD)[:, :, 0]
         )
+        group_sum_bf = held.tile([P, GROUPS], BF16, name="group_sum_bf")
+        nc.vector.tensor_copy(group_sum_bf[:], group_sum[:])
+        minus_ones = held.tile([P, P], BF16, name="minus_ones")
+        nc.vector.memset(minus_ones[:], -1.0)
 
         neg_mu = held.tile([P, N], F32, name="neg_mu")
         for piece in range(PIECES):
@@ -117,6 +121,29 @@ def tile_spnneuronbig_kernel(tc, x, means, stds, w1, offs, out):
             by_leaf(k[:]), by_leaf(k[:]), HALF_LOG_2PI, for_all_leaves(log_wsum[:]), ALU.subtract, ALU.subtract
         )
 
+        last_k = k[:, (M - 1) * COLS : M * COLS]
+        v_shift = held.tile([P, (M - 1) * COLS], F32, name="v_shift")
+        nc.vector.tensor_tensor(
+            v_shift[:].rearrange("p (m b) -> p m b", m=M - 1),
+            k[:, 0 : (M - 1) * COLS].rearrange("p (m b) -> p m b", m=M - 1),
+            last_k.unsqueeze(1).to_broadcast([P, M - 1, COLS]),
+            ALU.subtract,
+        )
+
+        blocks_a_bank = BANK // (N // CARD)
+        spread_k = held.tile([P, COLS, GROUPS], F32, name="spread_k")
+        nc.vector.tensor_tensor(
+            spread_k[:],
+            group_sum[:].unsqueeze(1).to_broadcast([P, COLS, GROUPS]),
+            last_k.unsqueeze(2).to_broadcast([P, COLS, GROUPS]),
+            ALU.mult,
+        )
+        spread_k_again = spread_k[:].rearrange("p b g -> p (b g)").unsqueeze(1).to_broadcast([P, blocks_a_bank, N // CARD])
+        spread_k_high = held.tile([P, blocks_a_bank, N // CARD], BF16, name="spread_k_high")
+        nc.vector.tensor_copy(spread_k_high[:], spread_k_again)
+        spread_k_low = held.tile([P, blocks_a_bank, N // CARD], BF16, name="spread_k_low")
+        nc.vector.tensor_tensor(spread_k_low[:], spread_k_again, spread_k_high[:], ALU.subtract)
+
         def square(s):
             return slice(s * P, (s + 1) * P)
 
@@ -129,6 +156,9 @@ def tile_spnneuronbig_kernel(tc, x, means, stds, w1, offs, out):
         weights = {}
         mix_products = held.tile([P, CHUNKS * WIDTH], F32, name="mix_products")
         low_sum = [low_sums.tile([P, BANK], F32, name="low_sum") for i in range(RESULT_BANKS)]
+        for i in range(RESULT_BANKS):
+            nc.tensor.matmul(low_sum[i][:], minus_ones[:], spread_k_high[:].rearrange("p a q -> p (a q)"), start=True, stop=False)
+            nc.tensor.matmul(low_sum[i][:], minus_ones[:], spread_k_low[:].rearrange("p a q -> p (a q)"), start=False, stop=False)
 
         def look_up_and_flip(chunk):
             b, piece = divmod(chunk, PIECES)
@@ -143,7 +173,7 @@ def tile_spnneuronbig_kernel(tc, x, means, stds, w1, offs, out):
             for s in range(SUBS):
                 nc.tensor.transpose(diff_t[:, square(s)], diff[:, square(s)], identity[:])
             diffs[chunk] = diff_t
-            halves[chunk] = ring.tile([P, M, PIECE], F32, name="half")
+            halves[chunk] = ring.tile([P, M, PIECE], BF16, name="half")
 
         def score(chunk, m):
             piece = chunk % PIECES
@@ -156,33 +186,24 @@ def tile_spnneuronbig_kernel(tc, x, means, stds, w1, offs, out):
         def smallest(chunk):
             piece = chunk % PIECES
             half = halves[chunk]
-            umin = ring.tile([P, PIECE], F32, name="umin")
-            for s in range(SUBS):
-                nc.vector.tensor_scalar_sub(umin[:, square(s)], half[:, 2, square(s)], column(k, 2, piece, s))
-            for m in (1, 0):
+            for m in range(M - 1):
                 for s in range(SUBS):
-                    nc.vector.scalar_tensor_tensor(
-                        umin[:, square(s)], half[:, m, square(s)], column(k, m, piece, s), umin[:, square(s)],
-                        ALU.subtract, ALU.min,
-                    )
-            for m in range(M):
-                nc.vector.tensor_sub(half[:, m, :], half[:, m, :], umin[:])
+                    nc.vector.tensor_scalar_sub(half[:, m, square(s)], half[:, m, square(s)], column(v_shift, m, piece, s))
+            vmin = ring.tile([P, PIECE], BF16, name="vmin")
+            nc.vector.tensor_tensor(vmin[:], half[:, 0, :], half[:, 1, :], ALU.min)
+            nc.vector.tensor_tensor(vmin[:], vmin[:], half[:, 2, :], ALU.min)
+            nc.vector.tensor_sub(half[:], half[:], vmin[:].unsqueeze(1).to_broadcast([P, M, PIECE]))
             for s in range(SUBS):
                 g = chunk * WIDTH + s * GROUPS
                 nc.tensor.matmul(
-                    low_sum[g // BANK][:, g % BANK : g % BANK + GROUPS], umin[:, square(s)], group_sum[:],
-                    start=True, stop=True,
+                    low_sum[g // BANK][:, g % BANK : g % BANK + GROUPS], vmin[:, square(s)], group_sum_bf[:],
+                    start=False, stop=(g % BANK == BANK - GROUPS),
                 )
 
         def weigh(chunk, m):
-            piece = chunk % PIECES
             if m == 0:
                 weights[chunk] = ring.tile([P, M, PIECE], BF16, name="weight")
-            for s in range(SUBS):
-                nc.scalar.activation(
-                    weights[chunk][:, m, square(s)], halves[chunk][:, m, square(s)], FUNC.Exp,
-                    bias=column(k, m, piece, s), scale=-1.0,
-                )
+            nc.scalar.activation(weights[chunk][:, m, :], halves[chunk][:, m, :], FUNC.Exp, scale=-1.0)
 
         def mix(chunk):
             mix_ps = mixes.tile([P, PIECE], F32, name="mix_ps")
@@ -217,7 +238,6 @@ def tile_spnneuronbig_kernel(tc, x, means, stds, w1, offs, out):
 
         nc.scalar.activation(mix_products[:], mix_products[:], FUNC.Ln)
         result = held.tile([P, CHUNKS * WIDTH], F32, name="result")
-        blocks_a_bank = BANK // (N // CARD)
         for i in range(RESULT_BANKS):
             nc.vector.tensor_sub(result[:, i * BANK : (i + 1) * BANK], mix_products[:, i * BANK : (i + 1) * BANK], low_sum[i][:])
             nc.sync.dma_start(

@@ -83,11 +83,14 @@ def tile_spnneuronbig_kernel(tc, x, means, stds, w1, offs, out):
 
         cols_ps = flipped.tile([P, PIECE], F32, name="cols_ps", tag="diff_t")
         nc.tensor.transpose(cols_ps[:, 0 : 3 * ROWS], rows[:], identity[0 : 3 * ROWS, 0 : 3 * ROWS])
-        cols = held.tile([P, 3 * ROWS], F32, name="cols")
-        nc.vector.tensor_copy(cols[:], cols_ps[:, 0 : 3 * ROWS])
-        sd = cols[:, 0:ROWS]
-        w = cols[:, ROWS : 2 * ROWS]
-        mean = cols[:, 2 * ROWS : 3 * ROWS]
+        positive = held.tile([P, ROWS + COLS], F32, name="positive")
+        nc.vector.tensor_copy(positive[:, 0:ROWS], cols_ps[:, 0:ROWS])
+        cols = held.tile([P, 2 * ROWS], F32, name="cols")
+        nc.vector.tensor_copy(cols[:], cols_ps[:, ROWS : 3 * ROWS])
+        sd = positive[:, 0:ROWS]
+        wsum = positive[:, ROWS : ROWS + COLS]
+        w = cols[:, 0:ROWS]
+        mean = cols[:, ROWS : 2 * ROWS]
 
         def by_leaf(ap):
             return ap.rearrange("p (m b) -> p m b", m=M)
@@ -109,17 +112,16 @@ def tile_spnneuronbig_kernel(tc, x, means, stds, w1, offs, out):
         nc.vector.tensor_tensor(by_leaf(k[:]), by_leaf(w), for_all_leaves(wmax[:]), ALU.subtract)
         exp_w = held.tile([P, M * COLS], F32, name="exp_w")
         nc.scalar.activation(exp_w[:], k[:], FUNC.Exp)
-        wsum = held.tile([P, COLS], F32, name="wsum")
-        nc.vector.tensor_add(wsum[:], exp_w[:, 0:COLS], exp_w[:, COLS : 2 * COLS])
-        nc.vector.tensor_add(wsum[:], wsum[:], exp_w[:, 2 * COLS : 3 * COLS])
-        log_wsum = held.tile([P, COLS], F32, name="log_wsum")
-        nc.scalar.activation(log_wsum[:], wsum[:], FUNC.Ln)
-        log_sd = held.tile([P, M * COLS], F32, name="log_sd")
-        nc.scalar.activation(log_sd[:], sd, FUNC.Ln)
-        nc.vector.tensor_sub(k[:], k[:], log_sd[:])
+        nc.gpsimd.tensor_add(wsum, exp_w[:, 0:COLS], exp_w[:, COLS : 2 * COLS])
+        nc.gpsimd.tensor_add(wsum, wsum, exp_w[:, 2 * COLS : 3 * COLS])
+        logs = held.tile([P, ROWS + COLS], F32, name="logs")
+        nc.scalar.activation(logs[:], positive[:], FUNC.Ln)
+        nc.vector.tensor_sub(k[:], k[:], logs[:, 0:ROWS])
         nc.vector.scalar_tensor_tensor(
-            by_leaf(k[:]), by_leaf(k[:]), HALF_LOG_2PI, for_all_leaves(log_wsum[:]), ALU.subtract, ALU.subtract
+            by_leaf(k[:]), by_leaf(k[:]), HALF_LOG_2PI, for_all_leaves(logs[:, ROWS : ROWS + COLS]), ALU.subtract, ALU.subtract
         )
+        table_back = held.tile([P, 1], F32, name="table_back")
+        nc.scalar.activation(table_back[:], logs[:, 0:1], FUNC.Exp)
 
         last_k = k[:, (M - 1) * COLS : M * COLS]
         v_shift = held.tile([P, (M - 1) * COLS], F32, name="v_shift")
@@ -154,6 +156,7 @@ def tile_spnneuronbig_kernel(tc, x, means, stds, w1, offs, out):
         diffs = {}
         halves = {}
         weights = {}
+        mix_banks = {}
         mix_products = held.tile([P, CHUNKS * WIDTH], F32, name="mix_products")
         low_sum = [low_sums.tile([P, BANK], F32, name="low_sum") for i in range(RESULT_BANKS)]
         for i in range(RESULT_BANKS):
@@ -203,19 +206,18 @@ def tile_spnneuronbig_kernel(tc, x, means, stds, w1, offs, out):
         def weigh(chunk, m):
             if m == 0:
                 weights[chunk] = ring.tile([P, M, PIECE], BF16, name="weight")
+                mix_banks[chunk] = mixes.tile([P, PIECE], F32, name="mix_ps")
             nc.scalar.activation(weights[chunk][:, m, :], halves[chunk][:, m, :], FUNC.Exp, scale=-1.0)
-
-        def mix(chunk):
-            mix_ps = mixes.tile([P, PIECE], F32, name="mix_ps")
             for s in range(SUBS):
-                for m in range(M):
-                    nc.tensor.matmul(
-                        mix_ps[:, square(s)], weights[chunk][:, m, square(s)], identity_bf[:],
-                        start=(m == 0), stop=(m == M - 1),
-                    )
+                nc.tensor.matmul(
+                    mix_banks[chunk][:, square(s)], weights[chunk][:, m, square(s)], identity_bf[:],
+                    start=(m == 0 and s == 0), stop=(m == M - 1 and s == SUBS - 1),
+                )
+
+        def multiply(chunk):
             nc.vector.tensor_reduce(
                 mix_products[:, chunk * WIDTH : (chunk + 1) * WIDTH],
-                mix_ps[:].rearrange("p (g t) -> p g t", t=CARD),
+                mix_banks[chunk][:].rearrange("p (g t) -> p g t", t=CARD),
                 mybir.AxisListType.X,
                 ALU.mult,
             )
@@ -223,24 +225,24 @@ def tile_spnneuronbig_kernel(tc, x, means, stds, w1, offs, out):
         def is_chunk(chunk):
             return 0 <= chunk < CHUNKS
 
-        for step in range(CHUNKS + 3):
-            if is_chunk(step - 3):
-                mix(step - 3)
-            if is_chunk(step):
-                look_up_and_flip(step)
+        for step in range(-1, CHUNKS + 5):
+            if is_chunk(step - 4):
+                multiply(step - 4)
+            if is_chunk(step + 1):
+                look_up_and_flip(step + 1)
             for m in range(M):
                 if is_chunk(step):
                     score(step, m)
-                if is_chunk(step - 2):
-                    weigh(step - 2, m)
+                if is_chunk(step - 3):
+                    weigh(step - 3, m)
             if is_chunk(step - 1):
                 smallest(step - 1)
 
         nc.scalar.activation(mix_products[:], mix_products[:], FUNC.Ln)
         result = held.tile([P, CHUNKS * WIDTH], F32, name="result")
-        for i in range(RESULT_BANKS):
+        for i, queue in zip(range(RESULT_BANKS), (nc.sync, nc.scalar)):
             nc.vector.tensor_sub(result[:, i * BANK : (i + 1) * BANK], mix_products[:, i * BANK : (i + 1) * BANK], low_sum[i][:])
-            nc.sync.dma_start(
+            queue.dma_start(
                 out[i * blocks_a_bank * P : (i + 1) * blocks_a_bank * P, :].rearrange("(b p) q -> p b q", p=P),
                 result[:, i * BANK : (i + 1) * BANK].rearrange("p (b q) -> p b q", b=blocks_a_bank),
             )

@@ -11,7 +11,6 @@ FUNC = mybir.ActivationFunctionType
 
 P = 128
 C, S, N, M, CARD = 512, 4096, 1024, 3, 4
-HALF_LOG_2PI = 0.5 * math.log(2.0 * math.pi)
 
 BANK = 512
 BLOCKS = C // P
@@ -36,13 +35,8 @@ def tile_spnneuronbig_kernel(tc, x, means, stds, w1, offs, out):
         tc.psum_pool(name="mixes", bufs=3) as mixes,
         tc.psum_pool(name="low_sums", bufs=RESULT_BANKS) as low_sums,
     ):
-        rows = held.tile([3 * ROWS, P], F32, name="rows")
-        for i, parameter in enumerate((stds, w1, means)):
-            nc.sync.dma_start(rows[i * ROWS : (i + 1) * ROWS, :], parameter.rearrange("m (b p) -> (m b) p", p=P))
-
         offsets = held.tile([P, N // 16], U16, name="offsets")
         nc.sync.dma_start(offsets[:], offs)
-
         mu = held.tile([P, N], F32, name="mu")
         windows = [tables.tile([P, S], F32, name="window") for b in range(BLOCKS)]
 
@@ -55,6 +49,9 @@ def tile_spnneuronbig_kernel(tc, x, means, stds, w1, offs, out):
 
         load_means(0)
         load_block(0)
+        rows = held.tile([3 * ROWS, P], F32, name="rows")
+        for i, parameter in enumerate((stds, w1, means)):
+            nc.sync.dma_start(rows[i * ROWS : (i + 1) * ROWS, :], parameter.rearrange("m (b p) -> (m b) p", p=P))
         for piece in range(1, PIECES):
             load_means(piece)
         for b in range(1, BLOCKS):
@@ -62,19 +59,13 @@ def tile_spnneuronbig_kernel(tc, x, means, stds, w1, offs, out):
 
         identity = held.tile([P, P], F32, name="identity")
         make_identity(nc, identity[:])
-        identity_bf = held.tile([P, P], BF16, name="identity_bf")
-        nc.vector.tensor_copy(identity_bf[:], identity[:])
 
         blocks_of_ones = held.tile([P, P], F32, name="blocks_of_ones")
         make_block_diagonal(nc, blocks_of_ones[:], CARD)
-        group_sum = held.tile([P, GROUPS], F32, name="group_sum")
+        group_sum = held.tile([P, GROUPS], BF16, name="group_sum")
         nc.vector.tensor_copy(
             group_sum[:], blocks_of_ones[:].rearrange("p (g t) -> p g t", t=CARD)[:, :, 0]
         )
-        group_sum_bf = held.tile([P, GROUPS], BF16, name="group_sum_bf")
-        nc.vector.tensor_copy(group_sum_bf[:], group_sum[:])
-        minus_ones = held.tile([P, P], BF16, name="minus_ones")
-        nc.vector.memset(minus_ones[:], -1.0)
 
         neg_mu = held.tile([P, N], F32, name="neg_mu")
         for piece in range(PIECES):
@@ -83,14 +74,11 @@ def tile_spnneuronbig_kernel(tc, x, means, stds, w1, offs, out):
 
         cols_ps = flipped.tile([P, PIECE], F32, name="cols_ps", tag="diff_t")
         nc.tensor.transpose(cols_ps[:, 0 : 3 * ROWS], rows[:], identity[0 : 3 * ROWS, 0 : 3 * ROWS])
-        positive = held.tile([P, ROWS + COLS], F32, name="positive")
-        nc.vector.tensor_copy(positive[:, 0:ROWS], cols_ps[:, 0:ROWS])
-        cols = held.tile([P, 2 * ROWS], F32, name="cols")
-        nc.vector.tensor_copy(cols[:], cols_ps[:, ROWS : 3 * ROWS])
-        sd = positive[:, 0:ROWS]
-        wsum = positive[:, ROWS : ROWS + COLS]
-        w = cols[:, 0:ROWS]
-        mean = cols[:, ROWS : 2 * ROWS]
+        cols = held.tile([P, 3 * ROWS], F32, name="cols")
+        nc.vector.tensor_copy(cols[:], cols_ps[:, 0 : 3 * ROWS])
+        sd = cols[:, 0:ROWS]
+        w = cols[:, ROWS : 2 * ROWS]
+        mean = cols[:, 2 * ROWS : 3 * ROWS]
 
         def by_leaf(ap):
             return ap.rearrange("p (m b) -> p m b", m=M)
@@ -108,43 +96,16 @@ def tile_spnneuronbig_kernel(tc, x, means, stds, w1, offs, out):
         wmax = held.tile([P, COLS], F32, name="wmax")
         nc.vector.tensor_max(wmax[:], w[:, 0:COLS], w[:, COLS : 2 * COLS])
         nc.vector.tensor_max(wmax[:], wmax[:], w[:, 2 * COLS : 3 * COLS])
-        k = held.tile([P, M * COLS], F32, name="k")
-        nc.vector.tensor_tensor(by_leaf(k[:]), by_leaf(w), for_all_leaves(wmax[:]), ALU.subtract)
         exp_w = held.tile([P, M * COLS], F32, name="exp_w")
-        nc.scalar.activation(exp_w[:], k[:], FUNC.Exp)
-        nc.gpsimd.tensor_add(wsum, exp_w[:, 0:COLS], exp_w[:, COLS : 2 * COLS])
-        nc.gpsimd.tensor_add(wsum, wsum, exp_w[:, 2 * COLS : 3 * COLS])
-        logs = held.tile([P, ROWS + COLS], F32, name="logs")
-        nc.scalar.activation(logs[:], positive[:], FUNC.Ln)
-        nc.vector.tensor_sub(k[:], k[:], logs[:, 0:ROWS])
-        nc.vector.scalar_tensor_tensor(
-            by_leaf(k[:]), by_leaf(k[:]), HALF_LOG_2PI, for_all_leaves(logs[:, ROWS : ROWS + COLS]), ALU.subtract, ALU.subtract
-        )
-        table_back = held.tile([P, 1], F32, name="table_back")
-        nc.scalar.activation(table_back[:], logs[:, 0:1], FUNC.Exp)
-
-        last_k = k[:, (M - 1) * COLS : M * COLS]
-        v_shift = held.tile([P, (M - 1) * COLS], F32, name="v_shift")
-        nc.vector.tensor_tensor(
-            v_shift[:].rearrange("p (m b) -> p m b", m=M - 1),
-            k[:, 0 : (M - 1) * COLS].rearrange("p (m b) -> p m b", m=M - 1),
-            last_k.unsqueeze(1).to_broadcast([P, M - 1, COLS]),
-            ALU.subtract,
-        )
-
-        blocks_a_bank = BANK // (N // CARD)
-        spread_k = held.tile([P, COLS, GROUPS], F32, name="spread_k")
-        nc.vector.tensor_tensor(
-            spread_k[:],
-            group_sum[:].unsqueeze(1).to_broadcast([P, COLS, GROUPS]),
-            last_k.unsqueeze(2).to_broadcast([P, COLS, GROUPS]),
-            ALU.mult,
-        )
-        spread_k_again = spread_k[:].rearrange("p b g -> p (b g)").unsqueeze(1).to_broadcast([P, blocks_a_bank, N // CARD])
-        spread_k_high = held.tile([P, blocks_a_bank, N // CARD], BF16, name="spread_k_high")
-        nc.vector.tensor_copy(spread_k_high[:], spread_k_again)
-        spread_k_low = held.tile([P, blocks_a_bank, N // CARD], BF16, name="spread_k_low")
-        nc.vector.tensor_tensor(spread_k_low[:], spread_k_again, spread_k_high[:], ALU.subtract)
+        nc.vector.tensor_tensor(by_leaf(exp_w[:]), by_leaf(w), for_all_leaves(wmax[:]), ALU.subtract)
+        nc.scalar.activation(exp_w[:], exp_w[:], FUNC.Exp)
+        wsum = held.tile([P, COLS], F32, name="wsum")
+        nc.vector.tensor_add(wsum[:], exp_w[:, 0:COLS], exp_w[:, COLS : 2 * COLS])
+        nc.vector.tensor_add(wsum[:], wsum[:], exp_w[:, 2 * COLS : 3 * COLS])
+        a = held.tile([P, M * COLS], F32, name="a")
+        nc.vector.tensor_tensor(by_leaf(a[:]), by_leaf(sd), for_all_leaves(wsum[:]), ALU.mult)
+        nc.vector.reciprocal(a[:], a[:])
+        nc.vector.tensor_mul(a[:], a[:], exp_w[:])
 
         def square(s):
             return slice(s * P, (s + 1) * P)
@@ -153,15 +114,19 @@ def tile_spnneuronbig_kernel(tc, x, means, stds, w1, offs, out):
             c = m * COLS + piece * SUBS + s
             return tile[:, c : c + 1]
 
+        weighted_identity = held.tile([P, PIECES, M, SUBS, P], BF16, name="weighted_identity")
+
+        def weight_identities(piece):
+            for m in range(M):
+                for s in range(SUBS):
+                    nc.vector.tensor_scalar_mul(weighted_identity[:, piece, m, s, :], identity[:], column(a, m, piece, s))
+
         diffs = {}
         halves = {}
         weights = {}
         mix_banks = {}
         mix_products = held.tile([P, CHUNKS * WIDTH], F32, name="mix_products")
         low_sum = [low_sums.tile([P, BANK], F32, name="low_sum") for i in range(RESULT_BANKS)]
-        for i in range(RESULT_BANKS):
-            nc.tensor.matmul(low_sum[i][:], minus_ones[:], spread_k_high[:].rearrange("p a q -> p (a q)"), start=True, stop=False)
-            nc.tensor.matmul(low_sum[i][:], minus_ones[:], spread_k_low[:].rearrange("p a q -> p (a q)"), start=False, stop=False)
 
         def look_up_and_flip(chunk):
             b, piece = divmod(chunk, PIECES)
@@ -187,20 +152,16 @@ def tile_spnneuronbig_kernel(tc, x, means, stds, w1, offs, out):
                 )
 
         def smallest(chunk):
-            piece = chunk % PIECES
             half = halves[chunk]
-            for m in range(M - 1):
-                for s in range(SUBS):
-                    nc.vector.tensor_scalar_sub(half[:, m, square(s)], half[:, m, square(s)], column(v_shift, m, piece, s))
-            vmin = ring.tile([P, PIECE], BF16, name="vmin")
-            nc.vector.tensor_tensor(vmin[:], half[:, 0, :], half[:, 1, :], ALU.min)
-            nc.vector.tensor_tensor(vmin[:], vmin[:], half[:, 2, :], ALU.min)
-            nc.vector.tensor_sub(half[:], half[:], vmin[:].unsqueeze(1).to_broadcast([P, M, PIECE]))
+            hmin = ring.tile([P, PIECE], BF16, name="hmin")
+            nc.vector.tensor_tensor(hmin[:], half[:, 0, :], half[:, 1, :], ALU.min)
+            nc.vector.tensor_tensor(hmin[:], hmin[:], half[:, 2, :], ALU.min)
+            nc.vector.tensor_sub(half[:], half[:], hmin[:].unsqueeze(1).to_broadcast([P, M, PIECE]))
             for s in range(SUBS):
                 g = chunk * WIDTH + s * GROUPS
                 nc.tensor.matmul(
-                    low_sum[g // BANK][:, g % BANK : g % BANK + GROUPS], vmin[:, square(s)], group_sum_bf[:],
-                    start=False, stop=(g % BANK == BANK - GROUPS),
+                    low_sum[g // BANK][:, g % BANK : g % BANK + GROUPS], hmin[:, square(s)], group_sum[:],
+                    start=True, stop=True,
                 )
 
         def weigh(chunk, m):
@@ -210,7 +171,8 @@ def tile_spnneuronbig_kernel(tc, x, means, stds, w1, offs, out):
             nc.scalar.activation(weights[chunk][:, m, :], halves[chunk][:, m, :], FUNC.Exp, scale=-1.0)
             for s in range(SUBS):
                 nc.tensor.matmul(
-                    mix_banks[chunk][:, square(s)], weights[chunk][:, m, square(s)], identity_bf[:],
+                    mix_banks[chunk][:, square(s)], weights[chunk][:, m, square(s)],
+                    weighted_identity[:, chunk % PIECES, m, s, :],
                     start=(m == 0 and s == 0), stop=(m == M - 1 and s == SUBS - 1),
                 )
 
@@ -225,21 +187,24 @@ def tile_spnneuronbig_kernel(tc, x, means, stds, w1, offs, out):
         def is_chunk(chunk):
             return 0 <= chunk < CHUNKS
 
-        for step in range(-1, CHUNKS + 5):
+        for step in range(-2, CHUNKS + 5):
+            if is_chunk(step + 2):
+                look_up_and_flip(step + 2)
+            if is_chunk(step - 1):
+                smallest(step - 1)
             if is_chunk(step - 4):
                 multiply(step - 4)
-            if is_chunk(step + 1):
-                look_up_and_flip(step + 1)
+            if 0 <= step - 1 < PIECES:
+                weight_identities(step - 1)
             for m in range(M):
                 if is_chunk(step):
                     score(step, m)
                 if is_chunk(step - 3):
                     weigh(step - 3, m)
-            if is_chunk(step - 1):
-                smallest(step - 1)
 
-        nc.scalar.activation(mix_products[:], mix_products[:], FUNC.Ln)
+        nc.scalar.activation(mix_products[:], mix_products[:], FUNC.Ln, scale=(2.0 * math.pi) ** (-CARD / 2))
         result = held.tile([P, CHUNKS * WIDTH], F32, name="result")
+        blocks_a_bank = BANK // (N // CARD)
         for i, queue in zip(range(RESULT_BANKS), (nc.sync, nc.scalar)):
             nc.vector.tensor_sub(result[:, i * BANK : (i + 1) * BANK], mix_products[:, i * BANK : (i + 1) * BANK], low_sum[i][:])
             queue.dma_start(

@@ -63,8 +63,8 @@ def tile_spnneuronbig_kernel(tc, x, means, stds, w1, offs, out):
         blocks_of_ones = held.tile([P, P], F32, name="blocks_of_ones")
         make_block_diagonal(nc, blocks_of_ones[:], CARD)
         group_sum = held.tile([P, GROUPS], BF16, name="group_sum")
-        nc.vector.tensor_copy(
-            group_sum[:], blocks_of_ones[:].rearrange("p (g t) -> p g t", t=CARD)[:, :, 0]
+        nc.vector.tensor_scalar_mul(
+            group_sum[:], blocks_of_ones[:].rearrange("p (g t) -> p g t", t=CARD)[:, :, 0], 0.5
         )
 
         neg_mu = held.tile([P, N], F32, name="neg_mu")
@@ -75,7 +75,7 @@ def tile_spnneuronbig_kernel(tc, x, means, stds, w1, offs, out):
         cols_ps = flipped.tile([P, PIECE], F32, name="cols_ps", tag="diff_t")
         nc.tensor.transpose(cols_ps[:, 0 : 3 * ROWS], rows[:], identity[0 : 3 * ROWS, 0 : 3 * ROWS])
         cols = held.tile([P, 3 * ROWS], F32, name="cols")
-        nc.vector.tensor_copy(cols[:], cols_ps[:, 0 : 3 * ROWS])
+        nc.scalar.copy(cols[:], cols_ps[:, 0 : 3 * ROWS])
         sd = cols[:, 0:ROWS]
         w = cols[:, ROWS : 2 * ROWS]
         mean = cols[:, 2 * ROWS : 3 * ROWS]
@@ -88,7 +88,6 @@ def tile_spnneuronbig_kernel(tc, x, means, stds, w1, offs, out):
 
         z_scale = held.tile([P, M * COLS], F32, name="z_scale")
         nc.vector.reciprocal(z_scale[:], sd)
-        nc.vector.tensor_scalar_mul(z_scale[:], z_scale[:], math.sqrt(0.5))
         z_shift = held.tile([P, M * COLS], F32, name="z_shift")
         nc.vector.tensor_tensor(by_leaf(z_shift[:]), for_all_leaves(mean[:, 0:COLS]), by_leaf(mean), ALU.subtract)
         nc.vector.tensor_mul(z_shift[:], z_shift[:], z_scale[:])
@@ -122,7 +121,7 @@ def tile_spnneuronbig_kernel(tc, x, means, stds, w1, offs, out):
                     nc.vector.tensor_scalar_mul(weighted_identity[:, piece, m, s, :], identity[:], column(a, m, piece, s))
 
         diffs = {}
-        halves = {}
+        scores = {}
         weights = {}
         mix_banks = {}
         mix_products = held.tile([P, CHUNKS * WIDTH], F32, name="mix_products")
@@ -141,22 +140,22 @@ def tile_spnneuronbig_kernel(tc, x, means, stds, w1, offs, out):
             for s in range(SUBS):
                 nc.tensor.transpose(diff_t[:, square(s)], diff[:, square(s)], identity[:])
             diffs[chunk] = diff_t
-            halves[chunk] = ring.tile([P, M, PIECE], BF16, name="half")
+            scores[chunk] = ring.tile([P, M, PIECE], BF16, name="h")
 
         def score(chunk, m):
             piece = chunk % PIECES
             for s in range(SUBS):
                 nc.scalar.activation(
-                    halves[chunk][:, m, square(s)], diffs[chunk][:, square(s)], FUNC.Square,
+                    scores[chunk][:, m, square(s)], diffs[chunk][:, square(s)], FUNC.Square,
                     bias=column(z_shift, m, piece, s), scale=column(z_scale, m, piece, s),
                 )
 
         def smallest(chunk):
-            half = halves[chunk]
+            h = scores[chunk]
             hmin = ring.tile([P, PIECE], BF16, name="hmin")
-            nc.vector.tensor_tensor(hmin[:], half[:, 0, :], half[:, 1, :], ALU.min)
-            nc.vector.tensor_tensor(hmin[:], hmin[:], half[:, 2, :], ALU.min)
-            nc.vector.tensor_sub(half[:], half[:], hmin[:].unsqueeze(1).to_broadcast([P, M, PIECE]))
+            nc.vector.tensor_tensor(hmin[:], h[:, 0, :], h[:, 1, :], ALU.min)
+            nc.vector.tensor_tensor(hmin[:], hmin[:], h[:, 2, :], ALU.min)
+            nc.vector.tensor_sub(h[:], h[:], hmin[:].unsqueeze(1).to_broadcast([P, M, PIECE]))
             for s in range(SUBS):
                 g = chunk * WIDTH + s * GROUPS
                 nc.tensor.matmul(
@@ -168,7 +167,7 @@ def tile_spnneuronbig_kernel(tc, x, means, stds, w1, offs, out):
             if m == 0:
                 weights[chunk] = ring.tile([P, M, PIECE], BF16, name="weight")
                 mix_banks[chunk] = mixes.tile([P, PIECE], F32, name="mix_ps")
-            nc.scalar.activation(weights[chunk][:, m, :], halves[chunk][:, m, :], FUNC.Exp, scale=-1.0)
+            nc.scalar.activation(weights[chunk][:, m, :], scores[chunk][:, m, :], FUNC.Exp, scale=-0.5)
             for s in range(SUBS):
                 nc.tensor.matmul(
                     mix_banks[chunk][:, square(s)], weights[chunk][:, m, square(s)],

@@ -22,7 +22,7 @@ ROWS = M * COLS
 GROUPS = P // CARD
 CHUNKS = BLOCKS * PIECES
 WIDTH = PIECE // CARD
-RESULT_BANKS = CHUNKS * WIDTH // BANK
+assert BLOCKS * WIDTH == BANK
 
 
 def tile_spnneuronbig_kernel(tc, x, means, stds, w1, offs, out):
@@ -33,7 +33,7 @@ def tile_spnneuronbig_kernel(tc, x, means, stds, w1, offs, out):
         tc.tile_pool(name="ring", bufs=CHUNKS) as ring,
         tc.psum_pool(name="flipped", bufs=3) as flipped,
         tc.psum_pool(name="mixes", bufs=3) as mixes,
-        tc.psum_pool(name="low_sums", bufs=RESULT_BANKS) as low_sums,
+        tc.psum_pool(name="low_sums", bufs=PIECES) as low_sums,
     ):
         offsets = held.tile([P, N // 16], U16, name="offsets")
         nc.sync.dma_start(offsets[:], offs)
@@ -124,8 +124,8 @@ def tile_spnneuronbig_kernel(tc, x, means, stds, w1, offs, out):
         scores = {}
         weights = {}
         mix_banks = {}
-        mix_products = held.tile([P, CHUNKS * WIDTH], F32, name="mix_products")
-        low_sum = [low_sums.tile([P, BANK], F32, name="low_sum") for i in range(RESULT_BANKS)]
+        mix_products = held.tile([P, PIECES, BANK], F32, name="mix_products")
+        low_sum = [low_sums.tile([P, BANK], F32, name="low_sum") for piece in range(PIECES)]
 
         def look_up_and_flip(chunk):
             b, piece = divmod(chunk, PIECES)
@@ -157,9 +157,9 @@ def tile_spnneuronbig_kernel(tc, x, means, stds, w1, offs, out):
             nc.vector.tensor_tensor(hmin[:], hmin[:], h[:, 2, :], ALU.min)
             nc.vector.tensor_sub(h[:], h[:], hmin[:].unsqueeze(1).to_broadcast([P, M, PIECE]))
             for s in range(SUBS):
-                g = chunk * WIDTH + s * GROUPS
+                g = (chunk // PIECES) * WIDTH + s * GROUPS
                 nc.tensor.matmul(
-                    low_sum[g // BANK][:, g % BANK : g % BANK + GROUPS], hmin[:, square(s)], group_sum[:],
+                    low_sum[chunk % PIECES][:, g : g + GROUPS], hmin[:, square(s)], group_sum[:],
                     start=True, stop=True,
                 )
 
@@ -177,7 +177,7 @@ def tile_spnneuronbig_kernel(tc, x, means, stds, w1, offs, out):
 
         def multiply(chunk):
             nc.vector.tensor_reduce(
-                mix_products[:, chunk * WIDTH : (chunk + 1) * WIDTH],
+                mix_products[:, chunk % PIECES, (chunk // PIECES) * WIDTH : (chunk // PIECES + 1) * WIDTH],
                 mix_banks[chunk][:].rearrange("p (g t) -> p g t", t=CARD),
                 mybir.AxisListType.X,
                 ALU.mult,
@@ -201,12 +201,13 @@ def tile_spnneuronbig_kernel(tc, x, means, stds, w1, offs, out):
                 if is_chunk(step - 3):
                     weigh(step - 3, m)
 
-        nc.scalar.activation(mix_products[:], mix_products[:], FUNC.Ln, scale=(2.0 * math.pi) ** (-CARD / 2))
-        result = held.tile([P, CHUNKS * WIDTH], F32, name="result")
-        blocks_a_bank = BANK // (N // CARD)
-        for i, queue in zip(range(RESULT_BANKS), (nc.sync, nc.scalar)):
-            nc.vector.tensor_sub(result[:, i * BANK : (i + 1) * BANK], mix_products[:, i * BANK : (i + 1) * BANK], low_sum[i][:])
+        result = held.tile([P, PIECES, BANK], F32, name="result")
+        for piece, queue in zip(range(PIECES), (nc.sync, nc.scalar)):
+            nc.scalar.activation(
+                mix_products[:, piece, :], mix_products[:, piece, :], FUNC.Ln, scale=(2.0 * math.pi) ** (-CARD / 2)
+            )
+            nc.vector.tensor_sub(result[:, piece, :], mix_products[:, piece, :], low_sum[piece][:])
             queue.dma_start(
-                out[i * blocks_a_bank * P : (i + 1) * blocks_a_bank * P, :].rearrange("(b p) q -> p b q", p=P),
-                result[:, i * BANK : (i + 1) * BANK].rearrange("p (b q) -> p b q", b=blocks_a_bank),
+                out.rearrange("(b p) q -> p b q", p=P)[:, :, piece * WIDTH : (piece + 1) * WIDTH],
+                result[:, piece, :].rearrange("p (b q) -> p b q", b=BLOCKS),
             )

@@ -150,6 +150,16 @@ def tile_spnneuronbig_kernel(tc, x, means, stds, w1, offs, out):
                     bias=column(z_shift, m, piece, s), scale=column(z_scale, m, piece, s),
                 )
 
+        def score_on_vector(chunk, m):
+            piece = chunk % PIECES
+            z = ring.tile([P, PIECE], F32, name="z")
+            for s in range(SUBS):
+                nc.vector.tensor_scalar(
+                    z[:, square(s)], diffs[chunk][:, square(s)],
+                    column(z_scale, m, piece, s), column(z_shift, m, piece, s), ALU.mult, ALU.add,
+                )
+            nc.vector.tensor_mul(scores[chunk][:, m, :], z[:], z[:])
+
         def smallest(chunk):
             h = scores[chunk]
             hmin = ring.tile([P, PIECE], BF16, name="hmin")
@@ -197,7 +207,10 @@ def tile_spnneuronbig_kernel(tc, x, means, stds, w1, offs, out):
                 weight_identities(step - 1)
             for m in range(M):
                 if is_chunk(step):
-                    score(step, m)
+                    if m == M - 1 and step % 2 == 1:
+                        score_on_vector(step, m)
+                    else:
+                        score(step, m)
                 if is_chunk(step - 3):
                     weigh(step - 3, m)
 

@@ -207,7 +207,7 @@ def tile_spnneuronbig_kernel(tc, x, means, stds, w1, offs, out):
                 weight_identities(step - 1)
             for m in range(M):
                 if is_chunk(step):
-                    if m == M - 1 and step % 2 == 1:
+                    if m == M - 1 and step % 4 == 1:
                         score_on_vector(step, m)
                     else:
                         score(step, m)

@@ -31,8 +31,9 @@ def tile_spnneuronbig_kernel(tc, x, means, stds, w1, offs, out):
         tc.tile_pool(name="held", bufs=1) as held,
         tc.tile_pool(name="tables", bufs=BLOCKS) as tables,
         tc.tile_pool(name="ring", bufs=CHUNKS) as ring,
-        tc.psum_pool(name="flipped", bufs=3) as flipped,
-        tc.psum_pool(name="mixes", bufs=3) as mixes,
+        tc.psum_pool(name="flipped", bufs=2) as flipped,
+        tc.psum_pool(name="gaps", bufs=2) as gaps,
+        tc.psum_pool(name="mixes", bufs=2) as mixes,
         tc.psum_pool(name="low_sums", bufs=PIECES) as low_sums,
     ):
         offsets = held.tile([P, N // 16], U16, name="offsets")
@@ -60,6 +61,11 @@ def tile_spnneuronbig_kernel(tc, x, means, stds, w1, offs, out):
         identity = held.tile([P, P], F32, name="identity")
         make_identity(nc, identity[:])
 
+        plus_identity = held.tile([P, P], BF16, name="plus_identity")
+        nc.vector.tensor_copy(plus_identity[:], identity[:])
+        minus_identity = held.tile([P, P], BF16, name="minus_identity")
+        nc.vector.tensor_scalar_mul(minus_identity[:], identity[:], -1.0)
+
         blocks_of_ones = held.tile([P, P], F32, name="blocks_of_ones")
         make_block_diagonal(nc, blocks_of_ones[:], CARD)
         group_sum = held.tile([P, GROUPS], BF16, name="group_sum")
@@ -70,7 +76,7 @@ def tile_spnneuronbig_kernel(tc, x, means, stds, w1, offs, out):
         neg_mu = held.tile([P, N], F32, name="neg_mu")
         for piece in range(PIECES):
             entries = slice(piece * PIECE, (piece + 1) * PIECE)
-            nc.vector.tensor_scalar_mul(neg_mu[:, entries], mu[:, entries], -1.0)
+            nc.scalar.mul(neg_mu[:, entries], mu[:, entries], -1.0)
 
         cols_ps = flipped.tile([P, PIECE], F32, name="cols_ps", tag="diff_t")
         nc.tensor.transpose(cols_ps[:, 0 : 3 * ROWS], rows[:], identity[0 : 3 * ROWS, 0 : 3 * ROWS])
@@ -118,10 +124,14 @@ def tile_spnneuronbig_kernel(tc, x, means, stds, w1, offs, out):
         def weight_identities(piece):
             for m in range(M):
                 for s in range(SUBS):
-                    nc.vector.tensor_scalar_mul(weighted_identity[:, piece, m, s, :], identity[:], column(a, m, piece, s))
+                    nc.vector.tensor_scalar_mul(
+                        weighted_identity[:, piece, m, s, :], plus_identity[:], column(a, m, piece, s)
+                    )
 
         diffs = {}
         scores = {}
+        gap_banks = {}
+        last_gaps = {}
         weights = {}
         mix_banks = {}
         mix_products = held.tile([P, PIECES, BANK], F32, name="mix_products")
@@ -147,7 +157,7 @@ def tile_spnneuronbig_kernel(tc, x, means, stds, w1, offs, out):
             for s in range(SUBS):
                 nc.scalar.activation(
                     scores[chunk][:, m, square(s)], diffs[chunk][:, square(s)], FUNC.Square,
-                    bias=column(z_shift, m, piece, s), scale=column(z_scale, m, piece, s),
+                    bias=column(z_shift, m, piece, s) if m > 0 else 0.0, scale=column(z_scale, m, piece, s),
                 )
 
         def score_on_vector(chunk, m):
@@ -165,7 +175,12 @@ def tile_spnneuronbig_kernel(tc, x, means, stds, w1, offs, out):
             hmin = ring.tile([P, PIECE], BF16, name="hmin")
             nc.vector.tensor_tensor(hmin[:], h[:, 0, :], h[:, 1, :], ALU.min)
             nc.vector.tensor_tensor(hmin[:], hmin[:], h[:, 2, :], ALU.min)
-            nc.vector.tensor_sub(h[:], h[:], hmin[:].unsqueeze(1).to_broadcast([P, M, PIECE]))
+            gap_banks[chunk] = gaps.tile([P, M - 1, PIECE], BF16, name="gap")
+            for m in range(M - 1):
+                nc.tensor.matmul(gap_banks[chunk][:, m, :], plus_identity[:], hmin[:], start=True, stop=False)
+                nc.tensor.matmul(gap_banks[chunk][:, m, :], minus_identity[:], h[:, m, :], start=False, stop=True)
+            last_gaps[chunk] = ring.tile([P, PIECE], BF16, name="last_gap")
+            nc.vector.tensor_sub(last_gaps[chunk][:], hmin[:], h[:, M - 1, :])
             for s in range(SUBS):
                 g = (chunk // PIECES) * WIDTH + s * GROUPS
                 nc.tensor.matmul(
@@ -177,7 +192,8 @@ def tile_spnneuronbig_kernel(tc, x, means, stds, w1, offs, out):
             if m == 0:
                 weights[chunk] = ring.tile([P, M, PIECE], BF16, name="weight")
                 mix_banks[chunk] = mixes.tile([P, PIECE], F32, name="mix_ps")
-            nc.scalar.activation(weights[chunk][:, m, :], scores[chunk][:, m, :], FUNC.Exp, scale=-0.5)
+            gap = last_gaps[chunk][:] if m == M - 1 else gap_banks[chunk][:, m, :]
+            nc.scalar.activation(weights[chunk][:, m, :], gap, FUNC.Exp, scale=0.5)
             for s in range(SUBS):
                 nc.tensor.matmul(
                     mix_banks[chunk][:, square(s)], weights[chunk][:, m, square(s)],
@@ -207,7 +223,7 @@ def tile_spnneuronbig_kernel(tc, x, means, stds, w1, offs, out):
                 weight_identities(step - 1)
             for m in range(M):
                 if is_chunk(step):
-                    if m == M - 1 and step % 4 == 1:
+                    if m == M - 1 and step % 2 == 1:
                         score_on_vector(step, m)
                     else:
                         score(step, m)

@@ -36,27 +36,25 @@ def tile_spnneuronbig_kernel(tc, x, means, stds, w1, offs, out):
         tc.psum_pool(name="mixes", bufs=2) as mixes,
         tc.psum_pool(name="low_sums", bufs=PIECES) as low_sums,
     ):
+        early_rows = held.tile([P, P], F32, name="early_rows")
+        nc.gpsimd.memset(early_rows[:], 0.0)
+        late_rows = held.tile([P, P], F32, name="late_rows")
+        nc.gpsimd.memset(late_rows[:], 0.0)
+
+        def as_rows(ap):
+            return ap.rearrange("m (b p) -> (m b) p", p=P)
+
         offsets = held.tile([P, N // 16], U16, name="offsets")
         nc.sync.dma_start(offsets[:], offs)
-        mu = held.tile([P, N], F32, name="mu")
+        nc.sync.dma_start(early_rows[0:COLS, :], as_rows(means[0:1, :]))
+        for m in range(M):
+            nc.sync.dma_start(early_rows[(m + 1) * COLS : (m + 2) * COLS, :], as_rows(stds[m : m + 1, :]))
         windows = [tables.tile([P, S], F32, name="window") for b in range(BLOCKS)]
-
-        def load_means(piece):
-            entries = slice(piece * PIECE, (piece + 1) * PIECE)
-            nc.sync.dma_start(mu[:, entries], means[0, entries].partition_broadcast(P))
-
-        def load_block(b):
+        for b in range(BLOCKS):
             nc.sync.dma_start(windows[b][:], x[b * P : (b + 1) * P, :])
-
-        load_means(0)
-        load_block(0)
-        rows = held.tile([3 * ROWS, P], F32, name="rows")
-        for i, parameter in enumerate((stds, w1, means)):
-            nc.sync.dma_start(rows[i * ROWS : (i + 1) * ROWS, :], parameter.rearrange("m (b p) -> (m b) p", p=P))
-        for piece in range(1, PIECES):
-            load_means(piece)
-        for b in range(1, BLOCKS):
-            load_block(b)
+            if b == 0:
+                nc.sync.dma_start(late_rows[0:ROWS, :], as_rows(means))
+                nc.sync.dma_start(late_rows[ROWS : 2 * ROWS, :], as_rows(w1))
 
         identity = held.tile([P, P], F32, name="identity")
         make_identity(nc, identity[:])
@@ -73,18 +71,31 @@ def tile_spnneuronbig_kernel(tc, x, means, stds, w1, offs, out):
             group_sum[:], blocks_of_ones[:].rearrange("p (g t) -> p g t", t=CARD)[:, :, 0], 0.5
         )
 
+        def flip_rows(rows, count, name):
+            flipped_ps = flipped.tile([P, PIECE], F32, name="flipped_ps", tag="diff_t")
+            nc.tensor.transpose(flipped_ps[:, 0:P], rows[:], identity[:])
+            cols = held.tile([P, count], F32, name=name)
+            nc.scalar.copy(cols[:], flipped_ps[:, 0:count])
+            return cols
+
+        early_cols = flip_rows(early_rows, COLS + ROWS, "early_cols")
+        sd = early_cols[:, COLS : COLS + ROWS]
+
+        neg_mean = held.tile([P, COLS], F32, name="neg_mean")
+        nc.scalar.mul(neg_mean[:], early_cols[:, 0:COLS], -1.0)
         neg_mu = held.tile([P, N], F32, name="neg_mu")
         for piece in range(PIECES):
-            entries = slice(piece * PIECE, (piece + 1) * PIECE)
-            nc.scalar.mul(neg_mu[:, entries], mu[:, entries], -1.0)
+            neg_mu_ps = flipped.tile([P, PIECE], F32, name="neg_mu_ps", tag="diff_t")
+            for s in range(SUBS):
+                c = piece * SUBS + s
+                nc.tensor.transpose(
+                    neg_mu_ps[:, s * P : (s + 1) * P], neg_mean[:, c : c + 1].to_broadcast([P, P]), identity[:]
+                )
+            nc.scalar.copy(neg_mu[:, piece * PIECE : (piece + 1) * PIECE], neg_mu_ps[:])
 
-        cols_ps = flipped.tile([P, PIECE], F32, name="cols_ps", tag="diff_t")
-        nc.tensor.transpose(cols_ps[:, 0 : 3 * ROWS], rows[:], identity[0 : 3 * ROWS, 0 : 3 * ROWS])
-        cols = held.tile([P, 3 * ROWS], F32, name="cols")
-        nc.scalar.copy(cols[:], cols_ps[:, 0 : 3 * ROWS])
-        sd = cols[:, 0:ROWS]
-        w = cols[:, ROWS : 2 * ROWS]
-        mean = cols[:, 2 * ROWS : 3 * ROWS]
+        late_cols = flip_rows(late_rows, 2 * ROWS, "late_cols")
+        mean = late_cols[:, 0:ROWS]
+        w = late_cols[:, ROWS : 2 * ROWS]
 
         def by_leaf(ap):
             return ap.rearrange("p (m b) -> p m b", m=M)

@@ -18,7 +18,6 @@ PIECE = BANK
 PIECES = N // PIECE
 SUBS = PIECE // P
 COLS = N // P
-ROWS = M * COLS
 GROUPS = P // CARD
 CHUNKS = BLOCKS * PIECES
 WIDTH = PIECE // CARD
@@ -36,25 +35,18 @@ def tile_spnneuronbig_kernel(tc, x, means, stds, w1, offs, out):
         tc.psum_pool(name="mixes", bufs=2) as mixes,
         tc.psum_pool(name="low_sums", bufs=PIECES) as low_sums,
     ):
-        early_rows = held.tile([P, P], F32, name="early_rows")
-        nc.gpsimd.memset(early_rows[:], 0.0)
-        late_rows = held.tile([P, P], F32, name="late_rows")
-        nc.gpsimd.memset(late_rows[:], 0.0)
-
-        def as_rows(ap):
-            return ap.rearrange("m (b p) -> (m b) p", p=P)
-
+        rows = held.tile([P, M, P], F32, name="rows")
+        nc.vector.memset(rows[32:64, :, :], 0.0)
+        nc.gpsimd.memset(rows[64:P, :, :], 0.0)
+        for k, parameter in enumerate((means, stds, w1, w1)):
+            nc.sync.dma_start(
+                rows[k * COLS : (k + 1) * COLS, :, :], parameter.rearrange("m (b p) -> b m p", p=P)
+            )
         offsets = held.tile([P, N // 16], U16, name="offsets")
         nc.sync.dma_start(offsets[:], offs)
-        nc.sync.dma_start(early_rows[0:COLS, :], as_rows(means[0:1, :]))
-        for m in range(M):
-            nc.sync.dma_start(early_rows[(m + 1) * COLS : (m + 2) * COLS, :], as_rows(stds[m : m + 1, :]))
         windows = [tables.tile([P, S], F32, name="window") for b in range(BLOCKS)]
         for b in range(BLOCKS):
             nc.sync.dma_start(windows[b][:], x[b * P : (b + 1) * P, :])
-            if b == 0:
-                nc.sync.dma_start(late_rows[0:ROWS, :], as_rows(means))
-                nc.sync.dma_start(late_rows[ROWS : 2 * ROWS, :], as_rows(w1))
 
         identity = held.tile([P, P], F32, name="identity")
         make_identity(nc, identity[:])
@@ -71,18 +63,17 @@ def tile_spnneuronbig_kernel(tc, x, means, stds, w1, offs, out):
             group_sum[:], blocks_of_ones[:].rearrange("p (g t) -> p g t", t=CARD)[:, :, 0], 0.5
         )
 
-        def flip_rows(rows, count, name):
-            flipped_ps = flipped.tile([P, PIECE], F32, name="flipped_ps", tag="diff_t")
-            nc.tensor.transpose(flipped_ps[:, 0:P], rows[:], identity[:])
-            cols = held.tile([P, count], F32, name=name)
-            nc.scalar.copy(cols[:], flipped_ps[:, 0:count])
-            return cols
-
-        early_cols = flip_rows(early_rows, COLS + ROWS, "early_cols")
-        sd = early_cols[:, COLS : COLS + ROWS]
+        cols_ps = flipped.tile([P, M, P], F32, name="cols_ps", tag="diff_t")
+        for m in range(M):
+            nc.tensor.transpose(cols_ps[:, m, :], rows[:, m, :], identity[:])
+        cols = held.tile([P, M, 3 * COLS], F32, name="cols")
+        nc.scalar.copy(cols[:], cols_ps[:, :, 0 : 3 * COLS])
+        mean = cols[:, :, 0:COLS]
+        sd = cols[:, :, COLS : 2 * COLS]
+        w = cols[:, :, 2 * COLS : 3 * COLS]
 
         neg_mean = held.tile([P, COLS], F32, name="neg_mean")
-        nc.scalar.mul(neg_mean[:], early_cols[:, 0:COLS], -1.0)
+        nc.scalar.mul(neg_mean[:], mean[:, 0, :], -1.0)
         neg_mu = held.tile([P, N], F32, name="neg_mu")
         for piece in range(PIECES):
             neg_mu_ps = flipped.tile([P, PIECE], F32, name="neg_mu_ps", tag="diff_t")
@@ -93,33 +84,26 @@ def tile_spnneuronbig_kernel(tc, x, means, stds, w1, offs, out):
                 )
             nc.scalar.copy(neg_mu[:, piece * PIECE : (piece + 1) * PIECE], neg_mu_ps[:])
 
-        late_cols = flip_rows(late_rows, 2 * ROWS, "late_cols")
-        mean = late_cols[:, 0:ROWS]
-        w = late_cols[:, ROWS : 2 * ROWS]
-
-        def by_leaf(ap):
-            return ap.rearrange("p (m b) -> p m b", m=M)
-
         def for_all_leaves(ap):
             return ap.unsqueeze(1).to_broadcast([P, M, COLS])
 
-        z_scale = held.tile([P, M * COLS], F32, name="z_scale")
+        z_scale = held.tile([P, M, COLS], F32, name="z_scale")
         nc.vector.reciprocal(z_scale[:], sd)
-        z_shift = held.tile([P, M * COLS], F32, name="z_shift")
-        nc.vector.tensor_tensor(by_leaf(z_shift[:]), for_all_leaves(mean[:, 0:COLS]), by_leaf(mean), ALU.subtract)
+        z_shift = held.tile([P, M, COLS], F32, name="z_shift")
+        nc.vector.tensor_sub(z_shift[:], for_all_leaves(mean[:, 0, :]), mean)
         nc.vector.tensor_mul(z_shift[:], z_shift[:], z_scale[:])
 
         wmax = held.tile([P, COLS], F32, name="wmax")
-        nc.vector.tensor_max(wmax[:], w[:, 0:COLS], w[:, COLS : 2 * COLS])
-        nc.vector.tensor_max(wmax[:], wmax[:], w[:, 2 * COLS : 3 * COLS])
-        exp_w = held.tile([P, M * COLS], F32, name="exp_w")
-        nc.vector.tensor_tensor(by_leaf(exp_w[:]), by_leaf(w), for_all_leaves(wmax[:]), ALU.subtract)
+        nc.vector.tensor_max(wmax[:], w[:, 0, :], w[:, 1, :])
+        nc.vector.tensor_max(wmax[:], wmax[:], w[:, 2, :])
+        exp_w = held.tile([P, M, COLS], F32, name="exp_w")
+        nc.vector.tensor_sub(exp_w[:], w, for_all_leaves(wmax[:]))
         nc.scalar.activation(exp_w[:], exp_w[:], FUNC.Exp)
         wsum = held.tile([P, COLS], F32, name="wsum")
-        nc.vector.tensor_add(wsum[:], exp_w[:, 0:COLS], exp_w[:, COLS : 2 * COLS])
-        nc.vector.tensor_add(wsum[:], wsum[:], exp_w[:, 2 * COLS : 3 * COLS])
-        a = held.tile([P, M * COLS], F32, name="a")
-        nc.vector.tensor_tensor(by_leaf(a[:]), by_leaf(sd), for_all_leaves(wsum[:]), ALU.mult)
+        nc.vector.tensor_add(wsum[:], exp_w[:, 0, :], exp_w[:, 1, :])
+        nc.vector.tensor_add(wsum[:], wsum[:], exp_w[:, 2, :])
+        a = held.tile([P, M, COLS], F32, name="a")
+        nc.vector.tensor_mul(a[:], sd, for_all_leaves(wsum[:]))
         nc.vector.reciprocal(a[:], a[:])
         nc.vector.tensor_mul(a[:], a[:], exp_w[:])
 
@@ -127,8 +111,8 @@ def tile_spnneuronbig_kernel(tc, x, means, stds, w1, offs, out):
             return slice(s * P, (s + 1) * P)
 
         def column(tile, m, piece, s):
-            c = m * COLS + piece * SUBS + s
-            return tile[:, c : c + 1]
+            c = piece * SUBS + s
+            return tile[:, m, c : c + 1]
 
         weighted_identity = held.tile([P, PIECES, M, SUBS, P], BF16, name="weighted_identity")
 

@@ -132,26 +132,31 @@ def tile_spnneuronbig_kernel(tc, x, means, stds, w1, offs, out):
         mix_products = held.tile([P, PIECES, BANK], F32, name="mix_products")
         low_sum = [low_sums.tile([P, BANK], F32, name="low_sum") for piece in range(PIECES)]
 
-        def look_up_and_flip(chunk):
+        def look_up_and_flip(chunk, slots):
             b, piece = divmod(chunk, PIECES)
             diff = ring.tile([P, PIECE], F32, name="diff")
-            nc.vector.tensor_tensor(
-                diff[:],
-                windows[b][:].indirect(offsets[:, piece * (PIECE // 16) : (piece + 1) * (PIECE // 16)]),
-                neg_mu[:, piece * PIECE : (piece + 1) * PIECE],
-                ALU.add,
-            )
-            diff_t = flipped.tile([P, PIECE], F32, name="diff_t")
-            for s in range(SUBS):
-                nc.tensor.transpose(diff_t[:, square(s)], diff[:, square(s)], identity[:])
-            diffs[chunk] = diff_t
+            diffs[chunk] = []
+            part = PIECE // len(slots)
+            for i, (pool, tag) in enumerate(slots):
+                columns = slice(i * part, (i + 1) * part)
+                first = piece * PIECE + i * part
+                nc.vector.tensor_tensor(
+                    diff[:, columns],
+                    windows[b][:].indirect(offsets[:, first // 16 : (first + part) // 16]),
+                    neg_mu[:, first : first + part],
+                    ALU.add,
+                )
+                diff_t = pool.tile([P, part], F32, name="diff_t", tag=tag)
+                for s in range(part // P):
+                    nc.tensor.transpose(diff_t[:, square(s)], diff[:, square(i * part // P + s)], identity[:])
+                    diffs[chunk].append(diff_t[:, square(s)])
             scores[chunk] = ring.tile([P, M, PIECE], BF16, name="h")
 
         def score(chunk, m):
             piece = chunk % PIECES
             for s in range(SUBS):
                 nc.scalar.activation(
-                    scores[chunk][:, m, square(s)], diffs[chunk][:, square(s)], FUNC.Square,
+                    scores[chunk][:, m, square(s)], diffs[chunk][s], FUNC.Square,
                     bias=column(z_shift, m, piece, s) if m > 0 else 0.0, scale=column(z_scale, m, piece, s),
                 )
 
@@ -160,7 +165,7 @@ def tile_spnneuronbig_kernel(tc, x, means, stds, w1, offs, out):
             z = ring.tile([P, PIECE], F32, name="z")
             for s in range(SUBS):
                 nc.vector.tensor_scalar(
-                    z[:, square(s)], diffs[chunk][:, square(s)],
+                    z[:, square(s)], diffs[chunk][s],
                     column(z_scale, m, piece, s), column(z_shift, m, piece, s), ALU.mult, ALU.add,
                 )
             nc.vector.tensor_mul(scores[chunk][:, m, :], z[:], z[:])
@@ -207,11 +212,13 @@ def tile_spnneuronbig_kernel(tc, x, means, stds, w1, offs, out):
         def is_chunk(chunk):
             return 0 <= chunk < CHUNKS
 
-        for step in range(-2, CHUNKS + 5):
-            if is_chunk(step + 2):
-                look_up_and_flip(step + 2)
+        for step in range(-1, CHUNKS + 5):
             if is_chunk(step - 1):
                 smallest(step - 1)
+            if step + 1 == 0:
+                look_up_and_flip(0, [(flipped, "diff_t"), (mixes, "mix_ps")])
+            elif is_chunk(step + 1):
+                look_up_and_flip(step + 1, [(flipped, "diff_t")])
             if is_chunk(step - 4):
                 multiply(step - 4)
             if 0 <= step - 1 < PIECES:
@@ -226,11 +233,15 @@ def tile_spnneuronbig_kernel(tc, x, means, stds, w1, offs, out):
                     weigh(step - 3, m)
 
         result = held.tile([P, PIECES, BANK], F32, name="result")
+
+        def half_of(ap, half):
+            return ap.rearrange("p (b q) -> p b q", b=BLOCKS)[:, :, half * (WIDTH // 2) : (half + 1) * (WIDTH // 2)]
+
         for piece, queue in zip(range(PIECES), (nc.sync, nc.scalar)):
-            nc.scalar.activation(
-                mix_products[:, piece, :], mix_products[:, piece, :], FUNC.Ln, scale=(2.0 * math.pi) ** (-CARD / 2)
-            )
-            nc.vector.tensor_sub(result[:, piece, :], mix_products[:, piece, :], low_sum[piece][:])
+            for half in range(2):
+                products = half_of(mix_products[:, piece, :], half)
+                nc.scalar.activation(products, products, FUNC.Ln, scale=(2.0 * math.pi) ** (-CARD / 2))
+                nc.vector.tensor_sub(half_of(result[:, piece, :], half), products, half_of(low_sum[piece][:], half))
             queue.dma_start(
                 out.rearrange("(b p) q -> p b q", p=P)[:, :, piece * WIDTH : (piece + 1) * WIDTH],
                 result[:, piece, :].rearrange("p (b q) -> p b q", b=BLOCKS),

@@ -212,13 +212,13 @@ def tile_spnneuronbig_kernel(tc, x, means, stds, w1, offs, out):
         def is_chunk(chunk):
             return 0 <= chunk < CHUNKS
 
-        for step in range(-1, CHUNKS + 5):
+        for step in range(-2, CHUNKS + 5):
+            if step + 2 == 0:
+                look_up_and_flip(0, [(flipped, "diff_t"), (mixes, "mix_ps")])
+            elif is_chunk(step + 2):
+                look_up_and_flip(step + 2, [(flipped, "diff_t")])
             if is_chunk(step - 1):
                 smallest(step - 1)
-            if step + 1 == 0:
-                look_up_and_flip(0, [(flipped, "diff_t"), (mixes, "mix_ps")])
-            elif is_chunk(step + 1):
-                look_up_and_flip(step + 1, [(flipped, "diff_t")])
             if is_chunk(step - 4):
                 multiply(step - 4)
             if 0 <= step - 1 < PIECES:

import math

import concourse.mybir as mybir
from concourse.masks import make_block_diagonal, make_identity

F32 = mybir.dt.float32
BF16 = mybir.dt.bfloat16
U16 = mybir.dt.uint16
ALU = mybir.AluOpType
FUNC = mybir.ActivationFunctionType

P = 128
C, S, N, M, CARD = 512, 4096, 1024, 3, 4

BANK = 512
BLOCKS = C // P
PIECE = BANK
PIECES = N // PIECE
SUBS = PIECE // P
COLS = N // P
GROUPS = P // CARD
CHUNKS = BLOCKS * PIECES
WIDTH = PIECE // CARD
assert BLOCKS * WIDTH == BANK


def tile_spnneuronbig_kernel(tc, x, means, stds, w1, offs, out):
    nc = tc.nc
    with (
        tc.tile_pool(name="held", bufs=1) as held,
        tc.tile_pool(name="tables", bufs=BLOCKS) as tables,
        tc.tile_pool(name="ring", bufs=CHUNKS) as ring,
        tc.psum_pool(name="flipped", bufs=2) as flipped,
        tc.psum_pool(name="gaps", bufs=2) as gaps,
        tc.psum_pool(name="mixes", bufs=2) as mixes,
        tc.psum_pool(name="low_sums", bufs=PIECES) as low_sums,
    ):
        rows = held.tile([P, M, P], F32, name="rows")
        nc.vector.memset(rows[32:64, :, :], 0.0)
        nc.gpsimd.memset(rows[64:P, :, :], 0.0)
        for k, parameter in enumerate((means, stds, w1, w1)):
            nc.sync.dma_start(
                rows[k * COLS : (k + 1) * COLS, :, :], parameter.rearrange("m (b p) -> b m p", p=P)
            )
        offsets = held.tile([P, N // 16], U16, name="offsets")
        nc.sync.dma_start(offsets[:], offs)
        windows = [tables.tile([P, S], F32, name="window") for b in range(BLOCKS)]
        for b in range(BLOCKS):
            nc.sync.dma_start(windows[b][:], x[b * P : (b + 1) * P, :])

        identity = held.tile([P, P], F32, name="identity")
        make_identity(nc, identity[:])

        plus_identity = held.tile([P, P], BF16, name="plus_identity")
        nc.vector.tensor_copy(plus_identity[:], identity[:])
        minus_identity = held.tile([P, P], BF16, name="minus_identity")
        nc.vector.tensor_scalar_mul(minus_identity[:], identity[:], -1.0)

        blocks_of_ones = held.tile([P, P], F32, name="blocks_of_ones")
        make_block_diagonal(nc, blocks_of_ones[:], CARD)
        group_sum = held.tile([P, GROUPS], BF16, name="group_sum")
        nc.vector.tensor_scalar_mul(
            group_sum[:], blocks_of_ones[:].rearrange("p (g t) -> p g t", t=CARD)[:, :, 0], 0.5
        )

        cols_ps = flipped.tile([P, M, P], F32, name="cols_ps", tag="diff_t")
        for m in range(M):
            nc.tensor.transpose(cols_ps[:, m, :], rows[:, m, :], identity[:])
        cols = held.tile([P, M, 3 * COLS], F32, name="cols")
        nc.scalar.copy(cols[:], cols_ps[:, :, 0 : 3 * COLS])
        mean = cols[:, :, 0:COLS]
        sd = cols[:, :, COLS : 2 * COLS]
        w = cols[:, :, 2 * COLS : 3 * COLS]

        neg_mean = held.tile([P, COLS], F32, name="neg_mean")
        nc.scalar.mul(neg_mean[:], mean[:, 0, :], -1.0)
        neg_mu = held.tile([P, N], F32, name="neg_mu")
        for piece in range(PIECES):
            neg_mu_ps = flipped.tile([P, PIECE], F32, name="neg_mu_ps", tag="diff_t")
            for s in range(SUBS):
                c = piece * SUBS + s
                nc.tensor.transpose(
                    neg_mu_ps[:, s * P : (s + 1) * P], neg_mean[:, c : c + 1].to_broadcast([P, P]), identity[:]
                )
            nc.scalar.copy(neg_mu[:, piece * PIECE : (piece + 1) * PIECE], neg_mu_ps[:])

        def for_all_leaves(ap):
            return ap.unsqueeze(1).to_broadcast([P, M, COLS])

        z_scale = held.tile([P, M, COLS], F32, name="z_scale")
        nc.vector.reciprocal(z_scale[:], sd)
        z_shift = held.tile([P, M, COLS], F32, name="z_shift")
        nc.vector.tensor_sub(z_shift[:], for_all_leaves(mean[:, 0, :]), mean)
        nc.vector.tensor_mul(z_shift[:], z_shift[:], z_scale[:])

        wmax = held.tile([P, COLS], F32, name="wmax")
        nc.vector.tensor_max(wmax[:], w[:, 0, :], w[:, 1, :])
        nc.vector.tensor_max(wmax[:], wmax[:], w[:, 2, :])
        exp_w = held.tile([P, M, COLS], F32, name="exp_w")
        nc.vector.tensor_sub(exp_w[:], w, for_all_leaves(wmax[:]))
        nc.scalar.activation(exp_w[:], exp_w[:], FUNC.Exp)
        wsum = held.tile([P, COLS], F32, name="wsum")
        nc.vector.tensor_add(wsum[:], exp_w[:, 0, :], exp_w[:, 1, :])
        nc.vector.tensor_add(wsum[:], wsum[:], exp_w[:, 2, :])
        a = held.tile([P, M, COLS], F32, name="a")
        nc.vector.tensor_mul(a[:], sd, for_all_leaves(wsum[:]))
        nc.vector.reciprocal(a[:], a[:])
        nc.vector.tensor_mul(a[:], a[:], exp_w[:])

        def square(s):
            return slice(s * P, (s + 1) * P)

        def column(tile, m, piece, s):
            c = piece * SUBS + s
            return tile[:, m, c : c + 1]

        weighted_identity = held.tile([P, PIECES, M, SUBS, P], BF16, name="weighted_identity")

        def weight_identities(piece):
            for m in range(M):
                for s in range(SUBS):
                    nc.vector.tensor_scalar_mul(
                        weighted_identity[:, piece, m, s, :], plus_identity[:], column(a, m, piece, s)
                    )

        diffs = {}
        scores = {}
        gap_banks = {}
        last_gaps = {}
        weights = {}
        mix_banks = {}
        mix_products = held.tile([P, PIECES, BANK], F32, name="mix_products")
        low_sum = [low_sums.tile([P, BANK], F32, name="low_sum") for piece in range(PIECES)]

        def look_up_and_flip(chunk, slots):
            b, piece = divmod(chunk, PIECES)
            diff = ring.tile([P, PIECE], F32, name="diff")
            diffs[chunk] = []
            part = PIECE // len(slots)
            for i, (pool, tag) in enumerate(slots):
                columns = slice(i * part, (i + 1) * part)
                first = piece * PIECE + i * part
                nc.vector.tensor_tensor(
                    diff[:, columns],
                    windows[b][:].indirect(offsets[:, first // 16 : (first + part) // 16]),
                    neg_mu[:, first : first + part],
                    ALU.add,
                )
                diff_t = pool.tile([P, part], F32, name="diff_t", tag=tag)
                for s in range(part // P):
                    nc.tensor.transpose(diff_t[:, square(s)], diff[:, square(i * part // P + s)], identity[:])
                    diffs[chunk].append(diff_t[:, square(s)])
            scores[chunk] = ring.tile([P, M, PIECE], BF16, name="h")

        def score(chunk, m):
            piece = chunk % PIECES
            for s in range(SUBS):
                nc.scalar.activation(
                    scores[chunk][:, m, square(s)], diffs[chunk][s], FUNC.Square,
                    bias=column(z_shift, m, piece, s) if m > 0 else 0.0, scale=column(z_scale, m, piece, s),
                )

        def score_on_vector(chunk, m):
            piece = chunk % PIECES
            z = ring.tile([P, PIECE], F32, name="z")
            for s in range(SUBS):
                nc.vector.tensor_scalar(
                    z[:, square(s)], diffs[chunk][s],
                    column(z_scale, m, piece, s), column(z_shift, m, piece, s), ALU.mult, ALU.add,
                )
            nc.vector.tensor_mul(scores[chunk][:, m, :], z[:], z[:])

        def smallest(chunk):
            h = scores[chunk]
            hmin = ring.tile([P, PIECE], BF16, name="hmin")
            nc.vector.tensor_tensor(hmin[:], h[:, 0, :], h[:, 1, :], ALU.min)
            nc.vector.tensor_tensor(hmin[:], hmin[:], h[:, 2, :], ALU.min)
            gap_banks[chunk] = gaps.tile([P, M - 1, PIECE], BF16, name="gap")
            for m in range(M - 1):
                nc.tensor.matmul(gap_banks[chunk][:, m, :], plus_identity[:], hmin[:], start=True, stop=False)
                nc.tensor.matmul(gap_banks[chunk][:, m, :], minus_identity[:], h[:, m, :], start=False, stop=True)
            last_gaps[chunk] = ring.tile([P, PIECE], BF16, name="last_gap")
            nc.vector.tensor_sub(last_gaps[chunk][:], hmin[:], h[:, M - 1, :])
            for s in range(SUBS):
                g = (chunk // PIECES) * WIDTH + s * GROUPS
                nc.tensor.matmul(
                    low_sum[chunk % PIECES][:, g : g + GROUPS], hmin[:, square(s)], group_sum[:],
                    start=True, stop=True,
                )

        def weigh(chunk, m):
            if m == 0:
                weights[chunk] = ring.tile([P, M, PIECE], BF16, name="weight")
                mix_banks[chunk] = mixes.tile([P, PIECE], F32, name="mix_ps")
            gap = last_gaps[chunk][:] if m == M - 1 else gap_banks[chunk][:, m, :]
            nc.scalar.activation(weights[chunk][:, m, :], gap, FUNC.Exp, scale=0.5)
            for s in range(SUBS):
                nc.tensor.matmul(
                    mix_banks[chunk][:, square(s)], weights[chunk][:, m, square(s)],
                    weighted_identity[:, chunk % PIECES, m, s, :],
                    start=(m == 0 and s == 0), stop=(m == M - 1 and s == SUBS - 1),
                )

        def multiply(chunk):
            nc.vector.tensor_reduce(
                mix_products[:, chunk % PIECES, (chunk // PIECES) * WIDTH : (chunk // PIECES + 1) * WIDTH],
                mix_banks[chunk][:].rearrange("p (g t) -> p g t", t=CARD),
                mybir.AxisListType.X,
                ALU.mult,
            )

        def is_chunk(chunk):
            return 0 <= chunk < CHUNKS

        for step in range(-2, CHUNKS + 5):
            if step + 2 == 0:
                look_up_and_flip(0, [(flipped, "diff_t"), (mixes, "mix_ps")])
            elif is_chunk(step + 2):
                look_up_and_flip(step + 2, [(flipped, "diff_t")])
            if is_chunk(step - 1):
                smallest(step - 1)
            if is_chunk(step - 4):
                multiply(step - 4)
            if 0 <= step - 1 < PIECES:
                weight_identities(step - 1)
            for m in range(M):
                if is_chunk(step):
                    if m == M - 1 and step % 2 == 1:
                        score_on_vector(step, m)
                    else:
                        score(step, m)
                if is_chunk(step - 3):
                    weigh(step - 3, m)

        result = held.tile([P, PIECES, BANK], F32, name="result")

        def half_of(ap, half):
            return ap.rearrange("p (b q) -> p b q", b=BLOCKS)[:, :, half * (WIDTH // 2) : (half + 1) * (WIDTH // 2)]

        for piece, queue in zip(range(PIECES), (nc.sync, nc.scalar)):
            for half in range(2):
                products = half_of(mix_products[:, piece, :], half)
                nc.scalar.activation(products, products, FUNC.Ln, scale=(2.0 * math.pi) ** (-CARD / 2))
                nc.vector.tensor_sub(half_of(result[:, piece, :], half), products, half_of(low_sum[piece][:], half))
            queue.dma_start(
                out.rearrange("(b p) q -> p b q", p=P)[:, :, piece * WIDTH : (piece + 1) * WIDTH],
                result[:, piece, :].rearrange("p (b q) -> p b q", b=BLOCKS),
            )
